import numpy as np
import ml_dtypes


def mxq(x, axis, fmt="e4m3"):
    dtype, down = {"e4m3": (ml_dtypes.float8_e4m3fn, 7), "e5m2": (ml_dtypes.float8_e5m2, 14)}[fmt]
    v = np.moveaxis(np.asarray(x, np.float32).astype(ml_dtypes.bfloat16).astype(np.float64), axis, -1)
    blocks = v.reshape(v.shape[:-1] + (-1, 32))
    amax = np.abs(blocks).max(-1, keepdims=True)
    byte = np.maximum(np.where(amax > 0, np.frexp(amax)[1] - 1 + 127, 0) - down, 1)
    scale = np.exp2(byte - 127.0)
    codes = (blocks / scale).astype(np.float32).astype(dtype).astype(np.float64)
    return np.moveaxis((codes * scale).reshape(v.shape), -1, axis)


WIDE = False


def mx_kscale(k):
    if not WIDE:
        return np.ones(k)
    levels = np.array([10, -10, 5, -5, 0])
    a = np.random.permutation(np.resize(levels, k // 512 * 4)).reshape(k // 512, 4)
    idx = np.arange(k)
    return np.exp2(a[idx // 512, idx % 128 // 32])


BF16 = ml_dtypes.bfloat16


def bf(x):
    return np.asarray(x, np.float32).astype(BF16)


def f64(x):
    return np.asarray(x).astype(np.float64)


B, T, D = 8, 512, 1024
GAMMA = 0.5
EPS = 1e-06
REL_THRESH = 1e-09


def setup_inputs():
    s = mx_kscale(T)
    a = np.random.uniform(0.0, 1.0, (B, T, T))
    a = 0.5 * (a + a.transpose(0, 2, 1))
    k = np.random.standard_normal((B, T, D)) * np.sqrt(T)
    return {"A_rel": bf(a * s), "k_seq": bf(k * np.mean(s) / s[:, None])}


def reference(A_rel, k_seq):
    A = f64(A_rel)
    deg = np.sum(A, axis=-1) + EPS
    d_inv_sqrt = 1.0 / np.sqrt(deg)
    W = A * d_inv_sqrt[:, :, None] * d_inv_sqrt[:, None, :]
    n = A.shape[1]
    tril = np.tril(np.ones((n, n)))
    W_causal = W * tril
    a = mxq(W_causal, 2, "e4m3") @ mxq(f64(k_seq), 1, "e4m3")
    has_relation = np.max(np.abs(W) * tril, axis=-1) > REL_THRESH
    a_scaled = a * np.sqrt(GAMMA)
    out = a_scaled * has_relation[:, :, None].astype(np.float64)
    return out

@@ -1,0 +1,230 @@
+from contextlib import ExitStack
+import math
+
+import concourse.mybir as mybir
+from concourse.masks import make_identity
+
+F32 = mybir.dt.float32
+BF16 = mybir.dt.bfloat16
+U32 = mybir.dt.uint32
+U8 = mybir.dt.uint8
+I32 = mybir.dt.int32
+FP8X4 = mybir.dt.float8_e4m3fn_x4
+ALU = mybir.AluOpType
+ACT = mybir.ActivationFunctionType
+AX = mybir.AxisListType
+
+B, T, D = 8, 512, 1024
+P = 128
+NT = T // P
+HALF = 512
+EPS = 1e-06
+REL_THRESH = 1e-09
+GAMMA = 0.5
+FLOPS = 2 * B * T * T * D
+BYTES = B * T * T * 2 + B * T * D * 2 + B * T * D * 4
+
+A_PITCH = T + P
+W_OFF = (0, 128, 384, 768)
+N_G = 2
+VECTOR_OUT = ()
+
+
+def tile_symbolicpenaltytracker_t_kernel(tc, A_rel, k_seq, out):
+    nc = tc.nc
+    with ExitStack() as ctx:
+        const = ctx.enter_context(tc.tile_pool(name="const", bufs=1))
+        apool = ctx.enter_context(tc.tile_pool(name="apool", bufs=B))
+        kpool = ctx.enter_context(tc.tile_pool(name="kpool", bufs=B))
+        junkp = ctx.enter_context(tc.tile_pool(name="junkp", bufs=2))
+        small = ctx.enter_context(tc.tile_pool(name="small", bufs=4))
+        wpool = ctx.enter_context(tc.tile_pool(name="wpool", bufs=2))
+        cpool = ctx.enter_context(tc.tile_pool(name="cpool", bufs=3))
+        kgpool = ctx.enter_context(tc.tile_pool(name="kgpool", bufs=4))
+        opool = ctx.enter_context(tc.tile_pool(name="opool", bufs=10))
+        ps_b = ctx.enter_context(tc.psum_pool(name="ps_b", bufs=2))
+        ps_t = ctx.enter_context(tc.psum_pool(name="ps_t", bufs=2))
+        ps_o = ctx.enter_context(tc.psum_pool(name="ps_o", bufs=4))
+
+        a_tiles = []
+        k_tiles = []
+        for b in range(B):
+            a_t = apool.tile([P, NT * A_PITCH], BF16, name="a_t")
+            nc.sync.dma_start(
+                out=a_t[:, 0 : NT * T].rearrange("p (i s) -> p i s", i=NT),
+                in_=A_rel[b].rearrange("(i p) s -> p i s", p=P),
+            )
+            a_tiles.append(a_t)
+            k_t = kpool.tile([P, 4, D], BF16, name="k_t")
+            nc.sync.dma_start(out=k_t[:], in_=k_seq[b].rearrange("(j p) d -> p j d", p=P))
+            k_tiles.append(k_t)
+
+        ident = const.tile([P, P], F32, name="ident")
+        make_identity(nc, ident[:])
+        tri_f = const.tile([P, P], F32, name="tri_f")
+        nc.gpsimd.memset(tri_f[:], 1.0)
+        nc.gpsimd.affine_select(
+            out=tri_f[:],
+            in_=tri_f[:],
+            compare_op=ALU.is_ge,
+            fill=0.0,
+            base=0,
+            pattern=[[-1, P]],
+            channel_multiplier=1,
+        )
+        tri_b = const.tile([P, P], BF16, name="tri_b")
+        nc.vector.tensor_copy(out=tri_b[:], in_=tri_f[:])
+        eps_t = const.tile([P, 1], F32, name="eps_t")
+        nc.vector.memset(eps_t[:], EPS)
+        g_tiles = []
+        for n in range(N_G):
+            g_t = const.tile([P, NT, P, 4], BF16, name="g_t%d" % n, align_bytes=64)
+            nc.vector.memset(g_t[:], 0.0)
+            g_tiles.append(g_t)
+
+        def a_chain(b):
+            a_t = a_tiles[b]
+            deg = small.tile([P, NT], F32, name="deg")
+            for i in range(NT):
+                junk = junkp.tile([P, T], BF16, name="junk")
+                nc.scalar.activation(
+                    out=junk[:],
+                    in_=a_t[:, i * T : (i + 1) * T],
+                    func=ACT.Copy,
+                    accum_out=deg[:, i : i + 1],
+                )
+            root = small.tile([P, NT], F32, name="root")
+            nc.scalar.activation(out=root[:], in_=deg[:], func=ACT.Sqrt, bias=eps_t[:], scale=1.0)
+            dis = small.tile([P, NT], F32, name="dis")
+            nc.vector.reciprocal(out=dis[:], in_=root[:])
+            dis_b = ps_b.tile([P, T], F32, name="dis_b")
+            for i in range(NT):
+                nc.tensor.transpose(
+                    out=dis_b[:, i * P : (i + 1) * P],
+                    in_=dis[:, i : i + 1].to_broadcast([P, P]),
+                    identity=ident[:],
+                )
+            diag = a_t[:].rearrange("p (i c) -> p i c", c=A_PITCH)[:, :, 0:P]
+            nc.vector.tensor_tensor(
+                out=diag,
+                in0=diag,
+                in1=tri_b[:].unsqueeze(1).to_broadcast([P, NT, P]),
+                op=ALU.mult,
+            )
+            w_n = wpool.tile([P, 1280], F32, name="w_n")
+            peak = small.tile([P, NT], F32, name="peak")
+            for i in range(NT):
+                width = (i + 1) * P
+                w_i = w_n[:, W_OFF[i] : W_OFF[i] + width]
+                nc.vector.scalar_tensor_tensor(
+                    out=w_i,
+                    in0=a_t[:, i * T : i * T + width],
+                    scalar=dis[:, i : i + 1],
+                    in1=dis_b[:, 0:width],
+                    op0=ALU.mult,
+                    op1=ALU.mult,
+                )
+            w_abs = wpool.tile([P, 1280], F32, name="w_abs")
+            nc.vector.tensor_scalar(
+                out=w_abs[:].bitcast(I32),
+                in0=w_n[:].bitcast(I32),
+                scalar1=0x7FFFFFFF,
+                scalar2=None,
+                op0=ALU.bitwise_and,
+            )
+            for i in range(NT):
+                nc.vector.tensor_reduce(
+                    out=peak[:, i : i + 1],
+                    in_=w_abs[:, W_OFF[i] : W_OFF[i] + (i + 1) * P],
+                    axis=AX.X,
+                    op=ALU.max,
+                )
+            gain = small.tile([P, NT], F32, name="gain")
+            nc.vector.tensor_scalar(
+                out=gain[:],
+                in0=peak[:],
+                scalar1=REL_THRESH,
+                scalar2=math.sqrt(GAMMA),
+                op0=ALU.is_gt,
+                op1=ALU.mult,
+            )
+            g_t = g_tiles[b % N_G]
+            for i in range(NT):
+                w_t = ps_t.tile([P, 4, P], F32, name="w_t")
+                for j in range(i + 1):
+                    nc.tensor.transpose(
+                        out=w_t[:, j, :],
+                        in_=w_n[:, W_OFF[i] + j * P : W_OFF[i] + (j + 1) * P],
+                        identity=ident[:],
+                    )
+                nc.scalar.copy(
+                    out=g_t[:, i, :, 0 : i + 1],
+                    in_=w_t[:, 0 : i + 1, :].rearrange("p j t -> p t j"),
+                )
+            w_codes = cpool.tile([P, T], U32, name="w_codes", align_bytes=64)
+            w_scales = cpool.tile([P, T], U8, name="w_scales", align_bytes=64)
+            nc.vector.quantize_mx(
+                out=w_codes[:].bitcast(FP8X4),
+                scales=w_scales[:],
+                in_=g_t[:].rearrange("p i t j -> p (i t j)"),
+            )
+            return w_codes, w_scales, gain
+
+        def k_chain(b):
+            k_t = k_tiles[b]
+            k_codes = cpool.tile([P, D], U32, name="k_codes", align_bytes=64)
+            k_scales = cpool.tile([P, D], U8, name="k_scales", align_bytes=64)
+            grouped = []
+            for h in range(2):
+                k_g = kgpool.tile([P, HALF, 4], BF16, name="k_g", align_bytes=64)
+                nc.vector.tensor_copy(
+                    out=k_g[:].rearrange("p (c i) t -> p c t i", i=4),
+                    in_=k_t[:, :, h * HALF : (h + 1) * HALF].rearrange("p t (c i) -> p c t i", i=4),
+                )
+                grouped.append(k_g)
+            for h in range(2):
+                cols = slice(h * HALF, (h + 1) * HALF)
+                nc.vector.quantize_mx(
+                    out=k_codes[:, cols].bitcast(FP8X4),
+                    scales=k_scales[:, cols],
+                    in_=grouped[h][:].rearrange("p d t -> p (d t)"),
+                )
+            return k_codes, k_scales
+
+        def product(b, w_ops, k_ops):
+            w_codes, w_scales, gain = w_ops
+            k_codes, k_scales = k_ops
+            for i in range(NT):
+                rows = slice(i * P, (i + 1) * P)
+                o_t = opool.tile([P, D], F32, name="o_t")
+                for h in range(2):
+                    cols = slice(h * HALF, (h + 1) * HALF)
+                    acc = ps_o.tile([P, HALF], F32, name="acc")
+                    nc.tensor.matmul_mx(
+                        out=acc[:],
+                        lhsT=w_codes[:, rows].bitcast(FP8X4),
+                        lhsT_scale=w_scales[:, rows],
+                        rhs=k_codes[:, cols].bitcast(FP8X4),
+                        rhs_scale=k_scales[:, cols],
+                        start=True,
+                        stop=True,
+                    )
+                    if (i, h) in VECTOR_OUT:
+                        nc.vector.tensor_scalar(
+                            out=o_t[:, cols],
+                            in0=acc[:],
+                            scalar1=gain[:, i : i + 1],
+                            scalar2=None,
+                            op0=ALU.mult,
+                        )
+                    else:
+                        nc.scalar.activation(
+                            out=o_t[:, cols], in_=acc[:], func=ACT.Copy, scale=gain[:, i : i + 1]
+                        )
+                nc.sync.dma_start(out=out[b, rows, :], in_=o_t[:])
+
+        ready = {0: (a_chain(0), k_chain(0))}
+        for b in range(B):
+            if b + 1 < B:
+                ready[b + 1] = (a_chain(b + 1), k_chain(b + 1))
+            product(b, ready[b][0], ready[b][1])

@@ -27,6 +27,7 @@ BYTES = B * T * T * 2 + B * T * D * 2 + B * T * D * 4
 A_PITCH = T + P
 W_OFF = (0, 128, 384, 768)
 N_G = 2
+SCALAR_TEST = (3,)
 VECTOR_OUT = ()
 
 
@@ -37,14 +38,16 @@ def tile_symbolicpenaltytracker_t_kernel(tc, A_rel, k_seq, out):
         apool = ctx.enter_context(tc.tile_pool(name="apool", bufs=B))
         kpool = ctx.enter_context(tc.tile_pool(name="kpool", bufs=B))
         junkp = ctx.enter_context(tc.tile_pool(name="junkp", bufs=2))
+        atpool = ctx.enter_context(tc.tile_pool(name="atpool", bufs=2))
         small = ctx.enter_context(tc.tile_pool(name="small", bufs=4))
         wpool = ctx.enter_context(tc.tile_pool(name="wpool", bufs=2))
         cpool = ctx.enter_context(tc.tile_pool(name="cpool", bufs=3))
         kgpool = ctx.enter_context(tc.tile_pool(name="kgpool", bufs=4))
         opool = ctx.enter_context(tc.tile_pool(name="opool", bufs=10))
-        ps_b = ctx.enter_context(tc.psum_pool(name="ps_b", bufs=2))
+        ps_a = ctx.enter_context(tc.psum_pool(name="ps_a", bufs=2))
+        ps_b = ctx.enter_context(tc.psum_pool(name="ps_b", bufs=1))
         ps_t = ctx.enter_context(tc.psum_pool(name="ps_t", bufs=2))
-        ps_o = ctx.enter_context(tc.psum_pool(name="ps_o", bufs=4))
+        ps_o = ctx.enter_context(tc.psum_pool(name="ps_o", bufs=3))
 
         a_tiles = []
         k_tiles = []
@@ -76,6 +79,10 @@ def tile_symbolicpenaltytracker_t_kernel(tc, A_rel, k_seq, out):
         nc.vector.tensor_copy(out=tri_b[:], in_=tri_f[:])
         eps_t = const.tile([P, 1], F32, name="eps_t")
         nc.vector.memset(eps_t[:], EPS)
+        neg_thresh = const.tile([P, 1], F32, name="neg_thresh")
+        nc.vector.memset(neg_thresh[:], -REL_THRESH)
+        ones_b = const.tile([P, 2], BF16, name="ones_b")
+        nc.vector.memset(ones_b[:], 1.0)
         g_tiles = []
         for n in range(N_G):
             g_t = const.tile([P, NT, P, 4], BF16, name="g_t%d" % n, align_bytes=64)
@@ -84,20 +91,33 @@ def tile_symbolicpenaltytracker_t_kernel(tc, A_rel, k_seq, out):
 
         def a_chain(b):
             a_t = a_tiles[b]
-            deg = small.tile([P, NT], F32, name="deg")
+            a_words = a_t[:].bitcast(F32)
+            a_tr = atpool.tile([P, 2, T], F32, name="a_tr")
+            for u in range(2):
+                a_ps = ps_a.tile([P, NT, P], F32, name="a_ps")
+                for i in range(NT):
+                    first = i * (T // 2) + u * P
+                    nc.tensor.transpose(
+                        out=a_ps[:, i, :], in_=a_words[:, first : first + P], identity=ident[:]
+                    )
+                nc.scalar.copy(out=a_tr[:, u, :], in_=a_ps[:].rearrange("p i t -> p (i t)"))
+            a_halves = a_tr[:].bitcast(BF16).rearrange("p u (t e) -> p u t e", e=2)
+            dis_b = ps_b.tile([P, T], F32, name="dis_b")
             for i in range(NT):
-                junk = junkp.tile([P, T], BF16, name="junk")
-                nc.scalar.activation(
-                    out=junk[:],
-                    in_=a_t[:, i * T : (i + 1) * T],
-                    func=ACT.Copy,
-                    accum_out=deg[:, i : i + 1],
-                )
+                for j in range(NT):
+                    nc.tensor.matmul(
+                        out=dis_b[:, i : i + 1],
+                        lhsT=a_halves[:, j // 2, i * P : (i + 1) * P, j % 2],
+                        rhs=ones_b[:, 0:1],
+                        start=(j == 0),
+                        stop=(j == NT - 1),
+                    )
             root = small.tile([P, NT], F32, name="root")
-            nc.scalar.activation(out=root[:], in_=deg[:], func=ACT.Sqrt, bias=eps_t[:], scale=1.0)
+            nc.scalar.activation(
+                out=root[:], in_=dis_b[:, 0:NT], func=ACT.Sqrt, bias=eps_t[:], scale=1.0
+            )
             dis = small.tile([P, NT], F32, name="dis")
             nc.vector.reciprocal(out=dis[:], in_=root[:])
-            dis_b = ps_b.tile([P, T], F32, name="dis_b")
             for i in range(NT):
                 nc.tensor.transpose(
                     out=dis_b[:, i * P : (i + 1) * P],
@@ -132,22 +152,31 @@ def tile_symbolicpenaltytracker_t_kernel(tc, A_rel, k_seq, out):
                 scalar2=None,
                 op0=ALU.bitwise_and,
             )
-            for i in range(NT):
-                nc.vector.tensor_reduce(
-                    out=peak[:, i : i + 1],
-                    in_=w_abs[:, W_OFF[i] : W_OFF[i] + (i + 1) * P],
-                    axis=AX.X,
-                    op=ALU.max,
-                )
+            over = small.tile([P, NT], F32, name="over")
             gain = small.tile([P, NT], F32, name="gain")
-            nc.vector.tensor_scalar(
-                out=gain[:],
-                in0=peak[:],
-                scalar1=REL_THRESH,
-                scalar2=math.sqrt(GAMMA),
-                op0=ALU.is_gt,
-                op1=ALU.mult,
-            )
+            for i in range(NT):
+                w_a = w_abs[:, W_OFF[i] : W_OFF[i] + (i + 1) * P]
+                if i in SCALAR_TEST:
+                    junk = junkp.tile([P, T], BF16, name="junk")
+                    nc.scalar.activation(
+                        out=junk[:, 0 : (i + 1) * P],
+                        in_=w_a,
+                        func=ACT.Relu,
+                        bias=neg_thresh[:],
+                        scale=1.0,
+                        accum_out=over[:, i : i + 1],
+                    )
+                else:
+                    nc.vector.tensor_reduce(out=peak[:, i : i + 1], in_=w_a, axis=AX.X, op=ALU.max)
+            for cols, values, level in ((slice(0, 3), peak, REL_THRESH), (slice(3, 4), over, 0.0)):
+                nc.vector.tensor_scalar(
+                    out=gain[:, cols],
+                    in0=values[:, cols],
+                    scalar1=level,
+                    scalar2=math.sqrt(GAMMA),
+                    op0=ALU.is_gt,
+                    op1=ALU.mult,
+                )
             g_t = g_tiles[b % N_G]
             for i in range(NT):
                 w_t = ps_t.tile([P, 4, P], F32, name="w_t")

@@ -27,27 +27,24 @@ BYTES = B * T * T * 2 + B * T * D * 2 + B * T * D * 4
 A_PITCH = T + P
 W_OFF = (0, 128, 384, 768)
 N_G = 2
-SCALAR_TEST = (3,)
-VECTOR_OUT = ()
 
 
 def tile_symbolicpenaltytracker_t_kernel(tc, A_rel, k_seq, out):
     nc = tc.nc
     with ExitStack() as ctx:
+        ctx.enter_context(tc.manual_schedule())
         const = ctx.enter_context(tc.tile_pool(name="const", bufs=1))
         apool = ctx.enter_context(tc.tile_pool(name="apool", bufs=B))
         kpool = ctx.enter_context(tc.tile_pool(name="kpool", bufs=B))
         junkp = ctx.enter_context(tc.tile_pool(name="junkp", bufs=2))
-        atpool = ctx.enter_context(tc.tile_pool(name="atpool", bufs=2))
-        small = ctx.enter_context(tc.tile_pool(name="small", bufs=4))
+        small = ctx.enter_context(tc.tile_pool(name="small", bufs=3))
         wpool = ctx.enter_context(tc.tile_pool(name="wpool", bufs=2))
         cpool = ctx.enter_context(tc.tile_pool(name="cpool", bufs=3))
         kgpool = ctx.enter_context(tc.tile_pool(name="kgpool", bufs=4))
         opool = ctx.enter_context(tc.tile_pool(name="opool", bufs=10))
-        ps_a = ctx.enter_context(tc.psum_pool(name="ps_a", bufs=2))
         ps_b = ctx.enter_context(tc.psum_pool(name="ps_b", bufs=1))
-        ps_t = ctx.enter_context(tc.psum_pool(name="ps_t", bufs=2))
-        ps_o = ctx.enter_context(tc.psum_pool(name="ps_o", bufs=3))
+        ps_t = ctx.enter_context(tc.psum_pool(name="ps_t", bufs=3))
+        ps_o = ctx.enter_context(tc.psum_pool(name="ps_o", bufs=4))
 
         a_tiles = []
         k_tiles = []
@@ -81,179 +78,292 @@ def tile_symbolicpenaltytracker_t_kernel(tc, A_rel, k_seq, out):
         nc.vector.memset(eps_t[:], EPS)
         neg_thresh = const.tile([P, 1], F32, name="neg_thresh")
         nc.vector.memset(neg_thresh[:], -REL_THRESH)
-        ones_b = const.tile([P, 2], BF16, name="ones_b")
-        nc.vector.memset(ones_b[:], 1.0)
         g_tiles = []
         for n in range(N_G):
             g_t = const.tile([P, NT, P, 4], BF16, name="g_t%d" % n, align_bytes=64)
             nc.vector.memset(g_t[:], 0.0)
             g_tiles.append(g_t)
 
-        def a_chain(b):
-            a_t = a_tiles[b]
-            a_words = a_t[:].bitcast(F32)
-            a_tr = atpool.tile([P, 2, T], F32, name="a_tr")
-            for u in range(2):
-                a_ps = ps_a.tile([P, NT, P], F32, name="a_ps")
-                for i in range(NT):
-                    first = i * (T // 2) + u * P
-                    nc.tensor.transpose(
-                        out=a_ps[:, i, :], in_=a_words[:, first : first + P], identity=ident[:]
-                    )
-                nc.scalar.copy(out=a_tr[:, u, :], in_=a_ps[:].rearrange("p i t -> p (i t)"))
-            a_halves = a_tr[:].bitcast(BF16).rearrange("p u (t e) -> p u t e", e=2)
-            dis_b = ps_b.tile([P, T], F32, name="dis_b")
+        deg, root, dis, dis_b, w_n, w_abs, w_t = {}, {}, {}, {}, {}, {}, {}
+        mark, gain, w_ops, k_g, k_ops, acc, o_t = {}, {}, {}, {}, {}, {}, {}
+
+        def live(b):
+            return 0 <= b < B
+
+        def degrees(b):
+            if not live(b):
+                return
+            deg[b] = small.tile([P, NT], F32, name="deg")
             for i in range(NT):
-                for j in range(NT):
-                    nc.tensor.matmul(
-                        out=dis_b[:, i : i + 1],
-                        lhsT=a_halves[:, j // 2, i * P : (i + 1) * P, j % 2],
-                        rhs=ones_b[:, 0:1],
-                        start=(j == 0),
-                        stop=(j == NT - 1),
-                    )
-            root = small.tile([P, NT], F32, name="root")
-            nc.scalar.activation(
-                out=root[:], in_=dis_b[:, 0:NT], func=ACT.Sqrt, bias=eps_t[:], scale=1.0
-            )
-            dis = small.tile([P, NT], F32, name="dis")
-            nc.vector.reciprocal(out=dis[:], in_=root[:])
-            for i in range(NT):
-                nc.tensor.transpose(
-                    out=dis_b[:, i * P : (i + 1) * P],
-                    in_=dis[:, i : i + 1].to_broadcast([P, P]),
-                    identity=ident[:],
+                junk = junkp.tile([P, T // 2], F32, name="d_junk")
+                nc.vector.scalar_tensor_tensor(
+                    out=junk[:],
+                    in0=a_tiles[b][:, i * T : i * T + T // 2],
+                    scalar=1.0,
+                    in1=a_tiles[b][:, i * T + T // 2 : (i + 1) * T],
+                    op0=ALU.mult,
+                    op1=ALU.add,
+                    accum_out=deg[b][:, i : i + 1],
                 )
-            diag = a_t[:].rearrange("p (i c) -> p i c", c=A_PITCH)[:, :, 0:P]
+
+        def square_root(b):
+            if not live(b):
+                return
+            root[b] = small.tile([P, NT], F32, name="root")
+            nc.scalar.activation(
+                out=root[b][:], in_=deg[b][:], func=ACT.Sqrt, bias=eps_t[:], scale=1.0
+            )
+
+        def inverse_and_mask(b):
+            if not live(b):
+                return
+            dis[b] = small.tile([P, NT], F32, name="dis")
+            nc.vector.reciprocal(out=dis[b][:], in_=root[b][:])
+            diag = a_tiles[b][:].rearrange("p (i c) -> p i c", c=A_PITCH)[:, :, 0:P]
             nc.vector.tensor_tensor(
                 out=diag,
                 in0=diag,
                 in1=tri_b[:].unsqueeze(1).to_broadcast([P, NT, P]),
                 op=ALU.mult,
             )
-            w_n = wpool.tile([P, 1280], F32, name="w_n")
-            peak = small.tile([P, NT], F32, name="peak")
+
+        def spread(b):
+            if not live(b):
+                return
+            dis_b[b] = ps_b.tile([P, T], F32, name="dis_b")
+            for i in range(NT):
+                nc.tensor.transpose(
+                    out=dis_b[b][:, i * P : (i + 1) * P],
+                    in_=dis[b][:, i : i + 1].to_broadcast([P, P]),
+                    identity=ident[:],
+                )
+
+        def weights(b):
+            if not live(b):
+                return
+            w_n[b] = wpool.tile([P, 1280], F32, name="w_n")
             for i in range(NT):
                 width = (i + 1) * P
-                w_i = w_n[:, W_OFF[i] : W_OFF[i] + width]
                 nc.vector.scalar_tensor_tensor(
-                    out=w_i,
-                    in0=a_t[:, i * T : i * T + width],
-                    scalar=dis[:, i : i + 1],
-                    in1=dis_b[:, 0:width],
+                    out=w_n[b][:, W_OFF[i] : W_OFF[i] + width],
+                    in0=a_tiles[b][:, i * T : i * T + width],
+                    scalar=dis[b][:, i : i + 1],
+                    in1=dis_b[b][:, 0:width],
                     op0=ALU.mult,
                     op1=ALU.mult,
                 )
-            w_abs = wpool.tile([P, 1280], F32, name="w_abs")
+
+        def flip(b, tiles):
+            if not live(b):
+                return
+            for i in tiles:
+                w_t[(b, i)] = ps_t.tile([P, 4, P], F32, name="w_t")
+                for j in range(i + 1):
+                    nc.tensor.transpose(
+                        out=w_t[(b, i)][:, j, :],
+                        in_=w_n[b][:, W_OFF[i] + j * P : W_OFF[i] + (j + 1) * P],
+                        identity=ident[:],
+                    )
+
+        def group(b, tiles):
+            if not live(b):
+                return
+            for i in tiles:
+                nc.scalar.copy(
+                    out=g_tiles[b % N_G][:, i, :, 0 : i + 1],
+                    in_=w_t[(b, i)][:, 0 : i + 1, :].rearrange("p j t -> p t j"),
+                )
+
+        def magnitude(b):
+            if not live(b):
+                return
+            w_abs[b] = wpool.tile([P, 1280], F32, name="w_abs")
             nc.vector.tensor_scalar(
-                out=w_abs[:].bitcast(I32),
-                in0=w_n[:].bitcast(I32),
+                out=w_abs[b][:].bitcast(I32),
+                in0=w_n[b][:].bitcast(I32),
                 scalar1=0x7FFFFFFF,
                 scalar2=None,
                 op0=ALU.bitwise_and,
             )
-            over = small.tile([P, NT], F32, name="over")
-            gain = small.tile([P, NT], F32, name="gain")
+
+        def test(b, on_vector):
+            if not live(b):
+                return
+            mark[b] = small.tile([P, NT], F32, name="mark")
             for i in range(NT):
-                w_a = w_abs[:, W_OFF[i] : W_OFF[i] + (i + 1) * P]
-                if i in SCALAR_TEST:
-                    junk = junkp.tile([P, T], BF16, name="junk")
+                w_a = w_abs[b][:, W_OFF[i] : W_OFF[i] + (i + 1) * P]
+                if on_vector:
+                    nc.vector.tensor_reduce(out=mark[b][:, i : i + 1], in_=w_a, axis=AX.X, op=ALU.max)
+                else:
+                    junk = junkp.tile([P, T], BF16, name="x_junk")
                     nc.scalar.activation(
                         out=junk[:, 0 : (i + 1) * P],
                         in_=w_a,
                         func=ACT.Relu,
                         bias=neg_thresh[:],
                         scale=1.0,
-                        accum_out=over[:, i : i + 1],
+                        accum_out=mark[b][:, i : i + 1],
                     )
-                else:
-                    nc.vector.tensor_reduce(out=peak[:, i : i + 1], in_=w_a, axis=AX.X, op=ALU.max)
-            for cols, values, level in ((slice(0, 3), peak, REL_THRESH), (slice(3, 4), over, 0.0)):
-                nc.vector.tensor_scalar(
-                    out=gain[:, cols],
-                    in0=values[:, cols],
-                    scalar1=level,
-                    scalar2=math.sqrt(GAMMA),
-                    op0=ALU.is_gt,
-                    op1=ALU.mult,
-                )
-            g_t = g_tiles[b % N_G]
-            for i in range(NT):
-                w_t = ps_t.tile([P, 4, P], F32, name="w_t")
-                for j in range(i + 1):
-                    nc.tensor.transpose(
-                        out=w_t[:, j, :],
-                        in_=w_n[:, W_OFF[i] + j * P : W_OFF[i] + (j + 1) * P],
-                        identity=ident[:],
-                    )
-                nc.scalar.copy(
-                    out=g_t[:, i, :, 0 : i + 1],
-                    in_=w_t[:, 0 : i + 1, :].rearrange("p j t -> p t j"),
-                )
+
+        def row_gain(b, on_vector):
+            if not live(b):
+                return
+            gain[b] = small.tile([P, NT], F32, name="gain")
+            nc.vector.tensor_scalar(
+                out=gain[b][:],
+                in0=mark[b][:],
+                scalar1=(REL_THRESH if on_vector else 0.0),
+                scalar2=math.sqrt(GAMMA),
+                op0=ALU.is_gt,
+                op1=ALU.mult,
+            )
+
+        def quantise_w(b):
+            if not live(b):
+                return
             w_codes = cpool.tile([P, T], U32, name="w_codes", align_bytes=64)
             w_scales = cpool.tile([P, T], U8, name="w_scales", align_bytes=64)
             nc.vector.quantize_mx(
                 out=w_codes[:].bitcast(FP8X4),
                 scales=w_scales[:],
-                in_=g_t[:].rearrange("p i t j -> p (i t j)"),
+                in_=g_tiles[b % N_G][:].rearrange("p i t j -> p (i t j)"),
             )
-            return w_codes, w_scales, gain
+            w_ops[b] = (w_codes, w_scales)
 
-        def k_chain(b):
-            k_t = k_tiles[b]
+        def regroup_k(b, halves, on_scalar):
+            if not live(b):
+                return
+            for h in halves:
+                k_g[(b, h)] = kgpool.tile([P, HALF, 4], BF16, name="k_g", align_bytes=64)
+                dst = k_g[(b, h)][:].rearrange("p (c i) t -> p c t i", i=4)
+                src = k_tiles[b][:, :, h * HALF : (h + 1) * HALF].rearrange("p t (c i) -> p c t i", i=4)
+                if on_scalar:
+                    nc.scalar.copy(out=dst, in_=src)
+                else:
+                    nc.vector.tensor_copy(out=dst, in_=src)
+
+        def quantise_k(b):
+            if not live(b):
+                return
             k_codes = cpool.tile([P, D], U32, name="k_codes", align_bytes=64)
             k_scales = cpool.tile([P, D], U8, name="k_scales", align_bytes=64)
-            grouped = []
-            for h in range(2):
-                k_g = kgpool.tile([P, HALF, 4], BF16, name="k_g", align_bytes=64)
-                nc.vector.tensor_copy(
-                    out=k_g[:].rearrange("p (c i) t -> p c t i", i=4),
-                    in_=k_t[:, :, h * HALF : (h + 1) * HALF].rearrange("p t (c i) -> p c t i", i=4),
-                )
-                grouped.append(k_g)
             for h in range(2):
                 cols = slice(h * HALF, (h + 1) * HALF)
                 nc.vector.quantize_mx(
                     out=k_codes[:, cols].bitcast(FP8X4),
                     scales=k_scales[:, cols],
-                    in_=grouped[h][:].rearrange("p d t -> p (d t)"),
+                    in_=k_g[(b, h)][:].rearrange("p d t -> p (d t)"),
                 )
-            return k_codes, k_scales
+            k_ops[b] = (k_codes, k_scales)
 
-        def product(b, w_ops, k_ops):
-            w_codes, w_scales, gain = w_ops
-            k_codes, k_scales = k_ops
-            for i in range(NT):
-                rows = slice(i * P, (i + 1) * P)
-                o_t = opool.tile([P, D], F32, name="o_t")
-                for h in range(2):
-                    cols = slice(h * HALF, (h + 1) * HALF)
-                    acc = ps_o.tile([P, HALF], F32, name="acc")
-                    nc.tensor.matmul_mx(
-                        out=acc[:],
-                        lhsT=w_codes[:, rows].bitcast(FP8X4),
-                        lhsT_scale=w_scales[:, rows],
-                        rhs=k_codes[:, cols].bitcast(FP8X4),
-                        rhs_scale=k_scales[:, cols],
-                        start=True,
-                        stop=True,
+        def multiply(b, passes):
+            if not live(b):
+                return
+            for n in passes:
+                rows = slice((n // 2) * P, (n // 2 + 1) * P)
+                cols = slice((n % 2) * HALF, (n % 2 + 1) * HALF)
+                acc[(b, n)] = ps_o.tile([P, HALF], F32, name="acc")
+                nc.tensor.matmul_mx(
+                    out=acc[(b, n)][:],
+                    lhsT=w_ops[b][0][:, rows].bitcast(FP8X4),
+                    lhsT_scale=w_ops[b][1][:, rows],
+                    rhs=k_ops[b][0][:, cols].bitcast(FP8X4),
+                    rhs_scale=k_ops[b][1][:, cols],
+                    start=True,
+                    stop=True,
+                )
+
+        def leave(b, passes, on_vector):
+            if not live(b):
+                return
+            for n in passes:
+                i = n // 2
+                cols = slice((n % 2) * HALF, (n % 2 + 1) * HALF)
+                if (b, i) not in o_t:
+                    o_t[(b, i)] = opool.tile([P, D], F32, name="o_t")
+                if on_vector:
+                    nc.vector.tensor_scalar(
+                        out=o_t[(b, i)][:, cols],
+                        in0=acc[(b, n)][:],
+                        scalar1=gain[b][:, i : i + 1],
+                        scalar2=None,
+                        op0=ALU.mult,
                     )
-                    if (i, h) in VECTOR_OUT:
-                        nc.vector.tensor_scalar(
-                            out=o_t[:, cols],
-                            in0=acc[:],
-                            scalar1=gain[:, i : i + 1],
-                            scalar2=None,
-                            op0=ALU.mult,
-                        )
-                    else:
-                        nc.scalar.activation(
-                            out=o_t[:, cols], in_=acc[:], func=ACT.Copy, scale=gain[:, i : i + 1]
-                        )
-                nc.sync.dma_start(out=out[b, rows, :], in_=o_t[:])
+                else:
+                    nc.scalar.activation(
+                        out=o_t[(b, i)][:, cols],
+                        in_=acc[(b, n)][:],
+                        func=ACT.Copy,
+                        scale=gain[b][:, i : i + 1],
+                    )
 
-        ready = {0: (a_chain(0), k_chain(0))}
-        for b in range(B):
-            if b + 1 < B:
-                ready[b + 1] = (a_chain(b + 1), k_chain(b + 1))
-            product(b, ready[b][0], ready[b][1])
+        def store(b, tiles):
+            if not live(b):
+                return
+            for i in tiles:
+                nc.sync.dma_start(out=out[b, i * P : (i + 1) * P, :], in_=o_t[(b, i)][:])
+
+        degrees(0)
+        square_root(0)
+        regroup_k(0, (0,), True)
+        inverse_and_mask(0)
+        spread(0)
+        weights(0)
+        flip(0, (0, 1, 2))
+        group(0, (0,))
+        flip(0, (3,))
+        group(0, (1, 2, 3))
+        magnitude(0)
+        test(0, False)
+        regroup_k(0, (1,), False)
+        quantise_k(0)
+        quantise_w(0)
+        multiply(0, (0, 1, 2, 3))
+        row_gain(0, False)
+        degrees(1)
+        square_root(1)
+        regroup_k(1, (0, 1), False)
+
+        for k in range(B):
+            c = k + 1
+            last = k == B - 1
+            before_last = k == B - 2
+            inverse_and_mask(c)
+            spread(c)
+            if last:
+                leave(k, (0, 2), False)
+                leave(k, (1, 3), True)
+            else:
+                leave(k, (0, 1, 2, 3), False)
+            store(k, (0, 1))
+            multiply(k, (4, 5, 6, 7))
+            quantise_k(c)
+            if last:
+                leave(k, (4, 6), False)
+                leave(k, (5, 7), True)
+                store(k, (2, 3))
+                continue
+            leave(k, (4, 5), False)
+            store(k, (2,))
+            weights(c)
+            flip(c, (0, 1, 2))
+            group(c, (0,))
+            flip(c, (3,))
+            group(c, (1, 2, 3))
+            magnitude(c)
+            test(c, before_last)
+            degrees(c + 1)
+            quantise_w(c)
+            if before_last:
+                row_gain(c, True)
+                leave(k, (6,), False)
+                leave(k, (7,), True)
+            else:
+                leave(k, (6, 7), False)
+            store(k, (3,))
+            multiply(c, (0, 1, 2, 3))
+            square_root(c + 1)
+            if not before_last:
+                regroup_k(c + 1, (0,), False)
+                row_gain(c, False)
+                regroup_k(c + 1, (1,), False)

@@ -320,9 +320,10 @@ def tile_symbolicpenaltytracker_t_kernel(tc, A_rel, k_seq, out):
         quantise_w(0)
         multiply(0, (0, 1, 2, 3))
         row_gain(0, False)
+        regroup_k(1, (0,), True)
         degrees(1)
         square_root(1)
-        regroup_k(1, (0, 1), False)
+        regroup_k(1, (1,), False)
 
         for k in range(B):
             c = k + 1
@@ -336,13 +337,14 @@ def tile_symbolicpenaltytracker_t_kernel(tc, A_rel, k_seq, out):
             else:
                 leave(k, (0, 1, 2, 3), False)
             store(k, (0, 1))
-            multiply(k, (4, 5, 6, 7))
-            quantise_k(c)
             if last:
+                multiply(k, (4, 5, 6, 7))
                 leave(k, (4, 6), False)
                 leave(k, (5, 7), True)
                 store(k, (2, 3))
                 continue
+            multiply(k, (4, 5))
+            quantise_k(c)
             leave(k, (4, 5), False)
             store(k, (2,))
             weights(c)
@@ -350,6 +352,7 @@ def tile_symbolicpenaltytracker_t_kernel(tc, A_rel, k_seq, out):
             group(c, (0,))
             flip(c, (3,))
             group(c, (1, 2, 3))
+            multiply(k, (6, 7))
             magnitude(c)
             test(c, before_last)
             degrees(c + 1)

@@ -174,23 +174,26 @@ def tile_symbolicpenaltytracker_t_kernel(tc, A_rel, k_seq, out):
                     in_=w_t[(b, i)][:, 0 : i + 1, :].rearrange("p j t -> p t j"),
                 )
 
-        def magnitude(b):
+        def magnitude(b, first, end):
             if not live(b):
                 return
-            w_abs[b] = wpool.tile([P, 1280], F32, name="w_abs")
+            if b not in w_abs:
+                w_abs[b] = wpool.tile([P, 1280], F32, name="w_abs")
+            cols = slice(W_OFF[first], W_OFF[end - 1] + end * P)
             nc.vector.tensor_scalar(
-                out=w_abs[b][:].bitcast(I32),
-                in0=w_n[b][:].bitcast(I32),
+                out=w_abs[b][:, cols].bitcast(I32),
+                in0=w_n[b][:, cols].bitcast(I32),
                 scalar1=0x7FFFFFFF,
                 scalar2=None,
                 op0=ALU.bitwise_and,
             )
 
-        def test(b, on_vector):
+        def test(b, tiles, on_vector):
             if not live(b):
                 return
-            mark[b] = small.tile([P, NT], F32, name="mark")
-            for i in range(NT):
+            if b not in mark:
+                mark[b] = small.tile([P, NT], F32, name="mark")
+            for i in tiles:
                 w_a = w_abs[b][:, W_OFF[i] : W_OFF[i] + (i + 1) * P]
                 if on_vector:
                     nc.vector.tensor_reduce(out=mark[b][:, i : i + 1], in_=w_a, axis=AX.X, op=ALU.max)
@@ -205,30 +208,33 @@ def tile_symbolicpenaltytracker_t_kernel(tc, A_rel, k_seq, out):
                         accum_out=mark[b][:, i : i + 1],
                     )
 
-        def row_gain(b, on_vector):
+        def row_gain(b, first, end, on_vector):
             if not live(b):
                 return
-            gain[b] = small.tile([P, NT], F32, name="gain")
+            if b not in gain:
+                gain[b] = small.tile([P, NT], F32, name="gain")
             nc.vector.tensor_scalar(
-                out=gain[b][:],
-                in0=mark[b][:],
+                out=gain[b][:, first:end],
+                in0=mark[b][:, first:end],
                 scalar1=(REL_THRESH if on_vector else 0.0),
                 scalar2=math.sqrt(GAMMA),
                 op0=ALU.is_gt,
                 op1=ALU.mult,
             )
 
-        def quantise_w(b):
+        def quantise_w(b, first, end):
             if not live(b):
                 return
-            w_codes = cpool.tile([P, T], U32, name="w_codes", align_bytes=64)
-            w_scales = cpool.tile([P, T], U8, name="w_scales", align_bytes=64)
+            if b not in w_ops:
+                w_codes = cpool.tile([P, T], U32, name="w_codes", align_bytes=64)
+                w_scales = cpool.tile([P, T], U8, name="w_scales", align_bytes=64)
+                w_ops[b] = (w_codes, w_scales)
+            cols = slice(first * P, end * P)
             nc.vector.quantize_mx(
-                out=w_codes[:].bitcast(FP8X4),
-                scales=w_scales[:],
-                in_=g_tiles[b % N_G][:].rearrange("p i t j -> p (i t j)"),
+                out=w_ops[b][0][:, cols].bitcast(FP8X4),
+                scales=w_ops[b][1][:, cols],
+                in_=g_tiles[b % N_G][:, first:end].rearrange("p i t j -> p (i t j)"),
             )
-            w_ops[b] = (w_codes, w_scales)
 
         def regroup_k(b, halves, on_scalar):
             if not live(b):
@@ -313,36 +319,24 @@ def tile_symbolicpenaltytracker_t_kernel(tc, A_rel, k_seq, out):
         group(0, (0,))
         flip(0, (3,))
         group(0, (1, 2, 3))
-        magnitude(0)
-        test(0, False)
+        magnitude(0, 0, NT)
+        test(0, range(NT), False)
         regroup_k(0, (1,), False)
         quantise_k(0)
-        quantise_w(0)
+        quantise_w(0, 0, NT)
         multiply(0, (0, 1, 2, 3))
-        row_gain(0, False)
+        row_gain(0, 0, NT, False)
         regroup_k(1, (0,), True)
         degrees(1)
         square_root(1)
         regroup_k(1, (1,), False)
 
-        for k in range(B):
+        for k in range(B - 2):
             c = k + 1
-            last = k == B - 1
-            before_last = k == B - 2
             inverse_and_mask(c)
             spread(c)
-            if last:
-                leave(k, (0, 2), False)
-                leave(k, (1, 3), True)
-            else:
-                leave(k, (0, 1, 2, 3), False)
+            leave(k, (0, 1, 2, 3), False)
             store(k, (0, 1))
-            if last:
-                multiply(k, (4, 5, 6, 7))
-                leave(k, (4, 6), False)
-                leave(k, (5, 7), True)
-                store(k, (2, 3))
-                continue
             multiply(k, (4, 5))
             quantise_k(c)
             leave(k, (4, 5), False)
@@ -353,20 +347,61 @@ def tile_symbolicpenaltytracker_t_kernel(tc, A_rel, k_seq, out):
             flip(c, (3,))
             group(c, (1, 2, 3))
             multiply(k, (6, 7))
-            magnitude(c)
-            test(c, before_last)
+            magnitude(c, 0, NT)
+            test(c, range(NT), False)
             degrees(c + 1)
-            quantise_w(c)
-            if before_last:
-                row_gain(c, True)
-                leave(k, (6,), False)
-                leave(k, (7,), True)
-            else:
-                leave(k, (6, 7), False)
+            quantise_w(c, 0, NT)
+            leave(k, (6, 7), False)
             store(k, (3,))
             multiply(c, (0, 1, 2, 3))
             square_root(c + 1)
-            if not before_last:
-                regroup_k(c + 1, (0,), False)
-                row_gain(c, False)
-                regroup_k(c + 1, (1,), False)
+            regroup_k(c + 1, (0,), False)
+            row_gain(c, 0, NT, False)
+            regroup_k(c + 1, (1,), False)
+
+        k = B - 2
+        c = B - 1
+        inverse_and_mask(c)
+        spread(c)
+        leave(k, (0, 1, 2, 3), False)
+        store(k, (0, 1))
+        multiply(k, (4, 5))
+        quantise_k(c)
+        leave(k, (4, 5), False)
+        store(k, (2,))
+        weights(c)
+        flip(c, (0, 1, 2))
+        multiply(k, (6, 7))
+        group(c, (0,))
+        flip(c, (3,))
+
+        def finish_tile(i):
+            magnitude(c, i, i + 1)
+            test(c, (i,), True)
+            row_gain(c, i, i + 1, True)
+            quantise_w(c, i, i + 1)
+
+        finish_tile(0)
+        group(c, (1,))
+        leave(k, (6,), False)
+        finish_tile(1)
+        leave(k, (7,), False)
+        store(k, (3,))
+        multiply(c, (0, 1, 2, 3))
+        group(c, (2,))
+        finish_tile(2)
+        group(c, (3,))
+        leave(c, (0, 1), False)
+        store(c, (0,))
+        finish_tile(3)
+        multiply(c, (4, 5))
+        leave(c, (2,), False)
+        leave(c, (3,), True)
+        store(c, (1,))
+        multiply(c, (6, 7))
+        leave(c, (4,), False)
+        leave(c, (5,), True)
+        store(c, (2,))
+        leave(c, (6,), False)
+        leave(c, (7,), True)
+        store(c, (3,))

@@ -174,26 +174,24 @@ def tile_symbolicpenaltytracker_t_kernel(tc, A_rel, k_seq, out):
                     in_=w_t[(b, i)][:, 0 : i + 1, :].rearrange("p j t -> p t j"),
                 )
 
-        def magnitude(b, first, end):
+        def magnitude(b):
             if not live(b):
                 return
-            if b not in w_abs:
-                w_abs[b] = wpool.tile([P, 1280], F32, name="w_abs")
-            cols = slice(W_OFF[first], W_OFF[end - 1] + end * P)
-            nc.vector.tensor_scalar(
-                out=w_abs[b][:, cols].bitcast(I32),
-                in0=w_n[b][:, cols].bitcast(I32),
-                scalar1=0x7FFFFFFF,
-                scalar2=None,
-                op0=ALU.bitwise_and,
-            )
+            w_abs[b] = wpool.tile([P, 1280], F32, name="w_abs")
+            for cols in (slice(0, W_OFF[3]), slice(W_OFF[3], 1280)):
+                nc.vector.tensor_scalar(
+                    out=w_abs[b][:, cols].bitcast(I32),
+                    in0=w_n[b][:, cols].bitcast(I32),
+                    scalar1=0x7FFFFFFF,
+                    scalar2=None,
+                    op0=ALU.bitwise_and,
+                )
 
-        def test(b, tiles, on_vector):
+        def test(b, on_vector):
             if not live(b):
                 return
-            if b not in mark:
-                mark[b] = small.tile([P, NT], F32, name="mark")
-            for i in tiles:
+            mark[b] = small.tile([P, NT], F32, name="mark")
+            for i in range(NT):
                 w_a = w_abs[b][:, W_OFF[i] : W_OFF[i] + (i + 1) * P]
                 if on_vector:
                     nc.vector.tensor_reduce(out=mark[b][:, i : i + 1], in_=w_a, axis=AX.X, op=ALU.max)
@@ -208,33 +206,30 @@ def tile_symbolicpenaltytracker_t_kernel(tc, A_rel, k_seq, out):
                         accum_out=mark[b][:, i : i + 1],
                     )
 
-        def row_gain(b, first, end, on_vector):
+        def row_gain(b, on_vector):
             if not live(b):
                 return
-            if b not in gain:
-                gain[b] = small.tile([P, NT], F32, name="gain")
+            gain[b] = small.tile([P, NT], F32, name="gain")
             nc.vector.tensor_scalar(
-                out=gain[b][:, first:end],
-                in0=mark[b][:, first:end],
+                out=gain[b][:],
+                in0=mark[b][:],
                 scalar1=(REL_THRESH if on_vector else 0.0),
                 scalar2=math.sqrt(GAMMA),
                 op0=ALU.is_gt,
                 op1=ALU.mult,
             )
 
-        def quantise_w(b, first, end):
+        def quantise_w(b):
             if not live(b):
                 return
-            if b not in w_ops:
-                w_codes = cpool.tile([P, T], U32, name="w_codes", align_bytes=64)
-                w_scales = cpool.tile([P, T], U8, name="w_scales", align_bytes=64)
-                w_ops[b] = (w_codes, w_scales)
-            cols = slice(first * P, end * P)
+            w_codes = cpool.tile([P, T], U32, name="w_codes", align_bytes=64)
+            w_scales = cpool.tile([P, T], U8, name="w_scales", align_bytes=64)
             nc.vector.quantize_mx(
-                out=w_ops[b][0][:, cols].bitcast(FP8X4),
-                scales=w_ops[b][1][:, cols],
-                in_=g_tiles[b % N_G][:, first:end].rearrange("p i t j -> p (i t j)"),
+                out=w_codes[:].bitcast(FP8X4),
+                scales=w_scales[:],
+                in_=g_tiles[b % N_G][:].rearrange("p i t j -> p (i t j)"),
             )
+            w_ops[b] = (w_codes, w_scales)
 
         def regroup_k(b, halves, on_scalar):
             if not live(b):
@@ -319,24 +314,36 @@ def tile_symbolicpenaltytracker_t_kernel(tc, A_rel, k_seq, out):
         group(0, (0,))
         flip(0, (3,))
         group(0, (1, 2, 3))
-        magnitude(0, 0, NT)
-        test(0, range(NT), False)
+        magnitude(0)
+        test(0, False)
         regroup_k(0, (1,), False)
         quantise_k(0)
-        quantise_w(0, 0, NT)
+        quantise_w(0)
         multiply(0, (0, 1, 2, 3))
-        row_gain(0, 0, NT, False)
+        row_gain(0, False)
         regroup_k(1, (0,), True)
         degrees(1)
         square_root(1)
         regroup_k(1, (1,), False)
 
-        for k in range(B - 2):
+        for k in range(B):
             c = k + 1
+            last = k == B - 1
+            before_last = k == B - 2
             inverse_and_mask(c)
             spread(c)
-            leave(k, (0, 1, 2, 3), False)
+            if last:
+                leave(k, (0, 2), False)
+                leave(k, (1, 3), True)
+            else:
+                leave(k, (0, 1, 2, 3), False)
             store(k, (0, 1))
+            if last:
+                multiply(k, (4, 5, 6, 7))
+                leave(k, (4, 6), False)
+                leave(k, (5, 7), True)
+                store(k, (2, 3))
+                continue
             multiply(k, (4, 5))
             quantise_k(c)
             leave(k, (4, 5), False)
@@ -347,61 +354,20 @@ def tile_symbolicpenaltytracker_t_kernel(tc, A_rel, k_seq, out):
             flip(c, (3,))
             group(c, (1, 2, 3))
             multiply(k, (6, 7))
-            magnitude(c, 0, NT)
-            test(c, range(NT), False)
+            magnitude(c)
+            test(c, before_last)
             degrees(c + 1)
-            quantise_w(c, 0, NT)
-            leave(k, (6, 7), False)
+            quantise_w(c)
+            if before_last:
+                row_gain(c, True)
+                leave(k, (6,), False)
+                leave(k, (7,), True)
+            else:
+                leave(k, (6, 7), False)
             store(k, (3,))
             multiply(c, (0, 1, 2, 3))
             square_root(c + 1)
-            regroup_k(c + 1, (0,), False)
-            row_gain(c, 0, NT, False)
-            regroup_k(c + 1, (1,), False)
-
-        k = B - 2
-        c = B - 1
-        inverse_and_mask(c)
-        spread(c)
-        leave(k, (0, 1, 2, 3), False)
-        store(k, (0, 1))
-        multiply(k, (4, 5))
-        quantise_k(c)
-        leave(k, (4, 5), False)
-        store(k, (2,))
-        weights(c)
-        flip(c, (0, 1, 2))
-        multiply(k, (6, 7))
-        group(c, (0,))
-        flip(c, (3,))
-
-        def finish_tile(i):
-            magnitude(c, i, i + 1)
-            test(c, (i,), True)
-            row_gain(c, i, i + 1, True)
-            quantise_w(c, i, i + 1)
-
-        finish_tile(0)
-        group(c, (1,))
-        leave(k, (6,), False)
-        finish_tile(1)
-        leave(k, (7,), False)
-        store(k, (3,))
-        multiply(c, (0, 1, 2, 3))
-        group(c, (2,))
-        finish_tile(2)
-        group(c, (3,))
-        leave(c, (0, 1), False)
-        store(c, (0,))
-        finish_tile(3)
-        multiply(c, (4, 5))
-        leave(c, (2,), False)
-        leave(c, (3,), True)
-        store(c, (1,))
-        multiply(c, (6, 7))
-        leave(c, (4,), False)
-        leave(c, (5,), True)
-        store(c, (2,))
-        leave(c, (6,), False)
-        leave(c, (7,), True)
-        store(c, (3,))
+            if not before_last:
+                regroup_k(c + 1, (0,), False)
+                row_gain(c, False)
+                regroup_k(c + 1, (1,), False)

@@ -8,7 +8,6 @@ F32 = mybir.dt.float32
 BF16 = mybir.dt.bfloat16
 U32 = mybir.dt.uint32
 U8 = mybir.dt.uint8
-I32 = mybir.dt.int32
 FP8X4 = mybir.dt.float8_e4m3fn_x4
 ALU = mybir.AluOpType
 ACT = mybir.ActivationFunctionType
@@ -27,6 +26,8 @@ BYTES = B * T * T * 2 + B * T * D * 2 + B * T * D * 4
 A_PITCH = T + P
 W_OFF = (0, 128, 384, 768)
 N_G = 2
+G_COLS = 768
+G_STEP = 256
 
 
 def tile_symbolicpenaltytracker_t_kernel(tc, A_rel, k_seq, out):
@@ -40,8 +41,9 @@ def tile_symbolicpenaltytracker_t_kernel(tc, A_rel, k_seq, out):
         small = ctx.enter_context(tc.tile_pool(name="small", bufs=3))
         wpool = ctx.enter_context(tc.tile_pool(name="wpool", bufs=2))
         cpool = ctx.enter_context(tc.tile_pool(name="cpool", bufs=3))
-        kgpool = ctx.enter_context(tc.tile_pool(name="kgpool", bufs=4))
-        opool = ctx.enter_context(tc.tile_pool(name="opool", bufs=10))
+        kgpool = ctx.enter_context(tc.tile_pool(name="kgpool", bufs=1))
+        kvpool = ctx.enter_context(tc.tile_pool(name="kvpool", bufs=2))
+        opool = ctx.enter_context(tc.tile_pool(name="opool", bufs=14))
         ps_b = ctx.enter_context(tc.psum_pool(name="ps_b", bufs=1))
         ps_t = ctx.enter_context(tc.psum_pool(name="ps_t", bufs=3))
         ps_o = ctx.enter_context(tc.psum_pool(name="ps_o", bufs=4))
@@ -50,15 +52,29 @@ def tile_symbolicpenaltytracker_t_kernel(tc, A_rel, k_seq, out):
         k_tiles = []
         for b in range(B):
             a_t = apool.tile([P, NT * A_PITCH], BF16, name="a_t")
-            nc.sync.dma_start(
-                out=a_t[:, 0 : NT * T].rearrange("p (i s) -> p i s", i=NT),
-                in_=A_rel[b].rearrange("(i p) s -> p i s", p=P),
-            )
+            pieces = 2 if b == 0 else 1
+            for q in range(pieces):
+                n = NT // pieces
+                nc.sync.dma_start(
+                    out=a_t[:, q * n * T : (q + 1) * n * T].rearrange("p (i s) -> p i s", i=n),
+                    in_=A_rel[b, q * n * P : (q + 1) * n * P, :].rearrange("(i p) s -> p i s", p=P),
+                )
             a_tiles.append(a_t)
             k_t = kpool.tile([P, 4, D], BF16, name="k_t")
-            nc.sync.dma_start(out=k_t[:], in_=k_seq[b].rearrange("(j p) d -> p j d", p=P))
+            for q in range(pieces):
+                cols = slice(q * D // pieces, (q + 1) * D // pieces)
+                nc.sync.dma_start(
+                    out=k_t[:, :, cols], in_=k_seq[b, :, cols].rearrange("(j p) d -> p j d", p=P)
+                )
             k_tiles.append(k_t)
 
+        g_tiles = []
+        for n in range(N_G):
+            g_t = const.tile([P, NT, P, 4], BF16, name="g_t%d" % n, align_bytes=64)
+            nc.vector.memset(g_t[:].rearrange("p i t j -> p (i t j)").bitcast(U32), 0)
+            g_tiles.append(g_t)
+        eps_t = const.tile([P, 1], F32, name="eps_t")
+        nc.vector.memset(eps_t[:], EPS)
         ident = const.tile([P, P], F32, name="ident")
         make_identity(nc, ident[:])
         tri_f = const.tile([P, P], F32, name="tri_f")
@@ -74,51 +90,35 @@ def tile_symbolicpenaltytracker_t_kernel(tc, A_rel, k_seq, out):
         )
         tri_b = const.tile([P, P], BF16, name="tri_b")
         nc.vector.tensor_copy(out=tri_b[:], in_=tri_f[:])
-        eps_t = const.tile([P, 1], F32, name="eps_t")
-        nc.vector.memset(eps_t[:], EPS)
-        neg_thresh = const.tile([P, 1], F32, name="neg_thresh")
-        nc.vector.memset(neg_thresh[:], -REL_THRESH)
-        g_tiles = []
-        for n in range(N_G):
-            g_t = const.tile([P, NT, P, 4], BF16, name="g_t%d" % n, align_bytes=64)
-            nc.vector.memset(g_t[:], 0.0)
-            g_tiles.append(g_t)
 
-        deg, root, dis, dis_b, w_n, w_abs, w_t = {}, {}, {}, {}, {}, {}, {}
+        deg, root, dis, dis_b, w_n, w_t = {}, {}, {}, {}, {}, {}
         mark, gain, w_ops, k_g, k_ops, acc, o_t = {}, {}, {}, {}, {}, {}, {}
 
-        def live(b):
-            return 0 <= b < B
-
         def degrees(b):
-            if not live(b):
-                return
             deg[b] = small.tile([P, NT], F32, name="deg")
             for i in range(NT):
-                junk = junkp.tile([P, T // 2], F32, name="d_junk")
-                nc.vector.scalar_tensor_tensor(
+                junk = junkp.tile([P, T], BF16, name="d_junk")
+                nc.vector.tensor_scalar(
                     out=junk[:],
-                    in0=a_tiles[b][:, i * T : i * T + T // 2],
-                    scalar=1.0,
-                    in1=a_tiles[b][:, i * T + T // 2 : (i + 1) * T],
+                    in0=a_tiles[b][:, i * T : (i + 1) * T],
+                    scalar1=1.0,
+                    scalar2=None,
                     op0=ALU.mult,
                     op1=ALU.add,
                     accum_out=deg[b][:, i : i + 1],
                 )
 
         def square_root(b):
-            if not live(b):
-                return
             root[b] = small.tile([P, NT], F32, name="root")
             nc.scalar.activation(
                 out=root[b][:], in_=deg[b][:], func=ACT.Sqrt, bias=eps_t[:], scale=1.0
             )
 
-        def inverse_and_mask(b):
-            if not live(b):
-                return
+        def inverse(b):
             dis[b] = small.tile([P, NT], F32, name="dis")
             nc.vector.reciprocal(out=dis[b][:], in_=root[b][:])
+
+        def mask(b):
             diag = a_tiles[b][:].rearrange("p (i c) -> p i c", c=A_PITCH)[:, :, 0:P]
             nc.vector.tensor_tensor(
                 out=diag,
@@ -128,9 +128,7 @@ def tile_symbolicpenaltytracker_t_kernel(tc, A_rel, k_seq, out):
             )
 
         def spread(b):
-            if not live(b):
-                return
-            dis_b[b] = ps_b.tile([P, T], F32, name="dis_b")
+            dis_b[b] = ps_b.tile([P, T], F32, name="row")
             for i in range(NT):
                 nc.tensor.transpose(
                     out=dis_b[b][:, i * P : (i + 1) * P],
@@ -139,8 +137,6 @@ def tile_symbolicpenaltytracker_t_kernel(tc, A_rel, k_seq, out):
                 )
 
         def weights(b):
-            if not live(b):
-                return
             w_n[b] = wpool.tile([P, 1280], F32, name="w_n")
             for i in range(NT):
                 width = (i + 1) * P
@@ -154,8 +150,6 @@ def tile_symbolicpenaltytracker_t_kernel(tc, A_rel, k_seq, out):
                 )
 
         def flip(b, tiles):
-            if not live(b):
-                return
             for i in tiles:
                 w_t[(b, i)] = ps_t.tile([P, 4, P], F32, name="w_t")
                 for j in range(i + 1):
@@ -166,62 +160,35 @@ def tile_symbolicpenaltytracker_t_kernel(tc, A_rel, k_seq, out):
                     )
 
         def group(b, tiles):
-            if not live(b):
-                return
             for i in tiles:
                 nc.scalar.copy(
                     out=g_tiles[b % N_G][:, i, :, 0 : i + 1],
                     in_=w_t[(b, i)][:, 0 : i + 1, :].rearrange("p j t -> p t j"),
                 )
 
-        def magnitude(b):
-            if not live(b):
-                return
-            w_abs[b] = wpool.tile([P, 1280], F32, name="w_abs")
-            for cols in (slice(0, W_OFF[3]), slice(W_OFF[3], 1280)):
-                nc.vector.tensor_scalar(
-                    out=w_abs[b][:, cols].bitcast(I32),
-                    in0=w_n[b][:, cols].bitcast(I32),
-                    scalar1=0x7FFFFFFF,
-                    scalar2=None,
-                    op0=ALU.bitwise_and,
-                )
-
-        def test(b, on_vector):
-            if not live(b):
-                return
+        def largest(b):
             mark[b] = small.tile([P, NT], F32, name="mark")
             for i in range(NT):
-                w_a = w_abs[b][:, W_OFF[i] : W_OFF[i] + (i + 1) * P]
-                if on_vector:
-                    nc.vector.tensor_reduce(out=mark[b][:, i : i + 1], in_=w_a, axis=AX.X, op=ALU.max)
-                else:
-                    junk = junkp.tile([P, T], BF16, name="x_junk")
-                    nc.scalar.activation(
-                        out=junk[:, 0 : (i + 1) * P],
-                        in_=w_a,
-                        func=ACT.Relu,
-                        bias=neg_thresh[:],
-                        scale=1.0,
-                        accum_out=mark[b][:, i : i + 1],
-                    )
+                nc.vector.tensor_reduce(
+                    out=mark[b][:, i : i + 1],
+                    in_=w_n[b][:, W_OFF[i] : W_OFF[i] + (i + 1) * P],
+                    axis=AX.X,
+                    op=ALU.max,
+                    apply_absolute_value=True,
+                )
 
-        def row_gain(b, on_vector):
-            if not live(b):
-                return
+        def row_gain(b):
             gain[b] = small.tile([P, NT], F32, name="gain")
             nc.vector.tensor_scalar(
                 out=gain[b][:],
                 in0=mark[b][:],
-                scalar1=(REL_THRESH if on_vector else 0.0),
+                scalar1=REL_THRESH,
                 scalar2=math.sqrt(GAMMA),
                 op0=ALU.is_gt,
                 op1=ALU.mult,
             )
 
         def quantise_w(b):
-            if not live(b):
-                return
             w_codes = cpool.tile([P, T], U32, name="w_codes", align_bytes=64)
             w_scales = cpool.tile([P, T], U8, name="w_scales", align_bytes=64)
             nc.vector.quantize_mx(
@@ -231,39 +198,62 @@ def tile_symbolicpenaltytracker_t_kernel(tc, A_rel, k_seq, out):
             )
             w_ops[b] = (w_codes, w_scales)
 
-        def regroup_k(b, halves, on_scalar):
-            if not live(b):
-                return
-            for h in halves:
-                k_g[(b, h)] = kgpool.tile([P, HALF, 4], BF16, name="k_g", align_bytes=64)
-                dst = k_g[(b, h)][:].rearrange("p (c i) t -> p c t i", i=4)
-                src = k_tiles[b][:, :, h * HALF : (h + 1) * HALF].rearrange("p t (c i) -> p c t i", i=4)
-                if on_scalar:
-                    nc.scalar.copy(out=dst, in_=src)
-                else:
-                    nc.vector.tensor_copy(out=dst, in_=src)
+        def piece(b, c0):
+            if b == 0:
+                if b not in k_g:
+                    k_g[b] = kgpool.tile([P, D, 4], BF16, name="k_first", align_bytes=64)
+                return k_g[b], 0
+            if c0 < G_COLS:
+                if (b, 0) not in k_g:
+                    k_g[(b, 0)] = kgpool.tile([P, G_COLS, 4], BF16, name="k_pool", align_bytes=64)
+                return k_g[(b, 0)], 0
+            if (b, 1) not in k_g:
+                k_g[(b, 1)] = kvpool.tile([P, D - G_COLS, 4], BF16, name="k_vec", align_bytes=64)
+            return k_g[(b, 1)], G_COLS
 
-        def quantise_k(b):
-            if not live(b):
-                return
-            k_codes = cpool.tile([P, D], U32, name="k_codes", align_bytes=64)
-            k_scales = cpool.tile([P, D], U8, name="k_scales", align_bytes=64)
-            for h in range(2):
-                cols = slice(h * HALF, (h + 1) * HALF)
-                nc.vector.quantize_mx(
-                    out=k_codes[:, cols].bitcast(FP8X4),
-                    scales=k_scales[:, cols],
-                    in_=k_g[(b, h)][:].rearrange("p d t -> p (d t)"),
+        def regroup(b, engine, c0, c1):
+            tile, first = piece(b, c0)
+            dst = tile[:, c0 - first : c1 - first, :]
+            source = k_tiles[b][:, :, c0:c1]
+            if engine == "gpsimd":
+                nc.gpsimd.tensor_scalar(
+                    out=dst,
+                    in0=source.rearrange("p t c -> p c t"),
+                    scalar1=1.0,
+                    scalar2=0.0,
+                    op0=ALU.mult,
+                    op1=ALU.add,
                 )
-            k_ops[b] = (k_codes, k_scales)
-
-        def multiply(b, passes):
-            if not live(b):
                 return
+            dst = dst.rearrange("p (c i) t -> p c t i", i=4)
+            source = source.rearrange("p t (c i) -> p c t i", i=4)
+            if engine == "scalar":
+                nc.scalar.copy(out=dst, in_=source)
+            else:
+                nc.vector.tensor_copy(out=dst, in_=source)
+
+        def regroup_on_gpsimd(b):
+            for c0 in range(0, G_COLS, G_STEP):
+                regroup(b, "gpsimd", c0, c0 + G_STEP)
+
+        def quantise_k(b, ranges):
+            if b not in k_ops:
+                k_codes = cpool.tile([P, D], U32, name="k_codes", align_bytes=64)
+                k_scales = cpool.tile([P, D], U8, name="k_scales", align_bytes=64)
+                k_ops[b] = (k_codes, k_scales)
+            for c0, c1 in ranges:
+                tile, first = piece(b, c0)
+                nc.vector.quantize_mx(
+                    out=k_ops[b][0][:, c0:c1].bitcast(FP8X4),
+                    scales=k_ops[b][1][:, c0:c1],
+                    in_=tile[:, c0 - first : c1 - first, :].rearrange("p d t -> p (d t)"),
+                )
+
+        def multiply(b, passes, pool=ps_o, name="acc"):
             for n in passes:
                 rows = slice((n // 2) * P, (n // 2 + 1) * P)
                 cols = slice((n % 2) * HALF, (n % 2 + 1) * HALF)
-                acc[(b, n)] = ps_o.tile([P, HALF], F32, name="acc")
+                acc[(b, n)] = pool.tile([P, HALF], F32, name=name)
                 nc.tensor.matmul_mx(
                     out=acc[(b, n)][:],
                     lhsT=w_ops[b][0][:, rows].bitcast(FP8X4),
@@ -274,15 +264,13 @@ def tile_symbolicpenaltytracker_t_kernel(tc, A_rel, k_seq, out):
                     stop=True,
                 )
 
-        def leave(b, passes, on_vector):
-            if not live(b):
-                return
+        def leave(b, passes, engine):
             for n in passes:
                 i = n // 2
                 cols = slice((n % 2) * HALF, (n % 2 + 1) * HALF)
                 if (b, i) not in o_t:
                     o_t[(b, i)] = opool.tile([P, D], F32, name="o_t")
-                if on_vector:
+                if engine == "vector":
                     nc.vector.tensor_scalar(
                         out=o_t[(b, i)][:, cols],
                         in0=acc[(b, n)][:],
@@ -299,54 +287,44 @@ def tile_symbolicpenaltytracker_t_kernel(tc, A_rel, k_seq, out):
                     )
 
         def store(b, tiles):
-            if not live(b):
-                return
             for i in tiles:
                 nc.sync.dma_start(out=out[b, i * P : (i + 1) * P, :], in_=o_t[(b, i)][:])
 
         degrees(0)
         square_root(0)
-        regroup_k(0, (0,), True)
-        inverse_and_mask(0)
+        mask(0)
+        inverse(0)
         spread(0)
+        regroup_on_gpsimd(1)
+        regroup(0, "scalar", 0, HALF)
+        regroup(0, "vector", HALF, G_COLS)
         weights(0)
         flip(0, (0, 1, 2))
         group(0, (0,))
         flip(0, (3,))
         group(0, (1, 2, 3))
-        magnitude(0)
-        test(0, False)
-        regroup_k(0, (1,), False)
-        quantise_k(0)
-        quantise_w(0)
-        multiply(0, (0, 1, 2, 3))
-        row_gain(0, False)
-        regroup_k(1, (0,), True)
+        largest(0)
         degrees(1)
         square_root(1)
-        regroup_k(1, (1,), False)
+        regroup(0, "vector", G_COLS, D)
+        quantise_w(0)
+        quantise_k(0, ((0, HALF), (HALF, D)))
+        row_gain(0)
+        inverse(1)
+        multiply(0, (0, 1, 2, 3))
+        spread(1)
+        regroup(1, "vector", G_COLS, D)
+        mask(1)
 
-        for k in range(B):
+        for k in range(B - 2):
             c = k + 1
-            last = k == B - 1
-            before_last = k == B - 2
-            inverse_and_mask(c)
-            spread(c)
-            if last:
-                leave(k, (0, 2), False)
-                leave(k, (1, 3), True)
-            else:
-                leave(k, (0, 1, 2, 3), False)
+            n = k + 2
+            quantise_k(c, ((G_COLS, D), (0, HALF), (HALF, G_COLS)))
+            regroup_on_gpsimd(n)
+            leave(k, (0, 1, 2, 3), "scalar")
             store(k, (0, 1))
-            if last:
-                multiply(k, (4, 5, 6, 7))
-                leave(k, (4, 6), False)
-                leave(k, (5, 7), True)
-                store(k, (2, 3))
-                continue
             multiply(k, (4, 5))
-            quantise_k(c)
-            leave(k, (4, 5), False)
+            leave(k, (4, 5), "scalar")
             store(k, (2,))
             weights(c)
             flip(c, (0, 1, 2))
@@ -354,20 +332,43 @@ def tile_symbolicpenaltytracker_t_kernel(tc, A_rel, k_seq, out):
             flip(c, (3,))
             group(c, (1, 2, 3))
             multiply(k, (6, 7))
-            magnitude(c)
-            test(c, before_last)
-            degrees(c + 1)
-            quantise_w(c)
-            if before_last:
-                row_gain(c, True)
-                leave(k, (6,), False)
-                leave(k, (7,), True)
-            else:
-                leave(k, (6, 7), False)
+            largest(c)
+            degrees(n)
+            square_root(n)
+            leave(k, (6, 7), "scalar")
             store(k, (3,))
+            quantise_w(c)
+            inverse(n)
+            row_gain(c)
             multiply(c, (0, 1, 2, 3))
-            square_root(c + 1)
-            if not before_last:
-                regroup_k(c + 1, (0,), False)
-                row_gain(c, False)
-                regroup_k(c + 1, (1,), False)
+            spread(n)
+            regroup(n, "vector", G_COLS, D)
+            mask(n)
+
+        k, c = B - 2, B - 1
+        weights(c)
+        leave(k, (0, 1, 2, 3), "scalar")
+        store(k, (0, 1))
+        multiply(k, (4, 5))
+        flip(c, (0, 1, 2))
+        leave(k, (4,), "scalar")
+        group(c, (0,))
+        flip(c, (3,))
+        group(c, (1, 2, 3))
+        multiply(k, (6, 7))
+        largest(c)
+        quantise_k(c, ((0, HALF),))
+        leave(k, (5,), "vector")
+        store(k, (2,))
+        quantise_w(c)
+        row_gain(c)
+        leave(k, (6, 7), "scalar")
+        store(k, (3,))
+        quantise_k(c, ((HALF, G_COLS), (G_COLS, D)))
+        multiply(c, (0, 2, 4, 6))
+        multiply(c, (1, 3, 5), ps_t, "w_t")
+        multiply(c, (7,), ps_b, "row")
+        for i in range(NT):
+            leave(c, (2 * i + 1,), "vector")
+            leave(c, (2 * i,), "scalar")
+            store(c, (i,))

@@ -307,12 +307,12 @@ def tile_symbolicpenaltytracker_t_kernel(tc, A_rel, k_seq, out):
         degrees(1)
         square_root(1)
         regroup(0, "vector", G_COLS, D)
-        quantise_w(0)
         quantise_k(0, ((0, HALF), (HALF, D)))
-        row_gain(0)
         inverse(1)
-        multiply(0, (0, 1, 2, 3))
         spread(1)
+        quantise_w(0)
+        row_gain(0)
+        multiply(0, (0, 1, 2, 3))
         regroup(1, "vector", G_COLS, D)
         mask(1)
 
@@ -324,24 +324,24 @@ def tile_symbolicpenaltytracker_t_kernel(tc, A_rel, k_seq, out):
             leave(k, (0, 1, 2, 3), "scalar")
             store(k, (0, 1))
             multiply(k, (4, 5))
+            degrees(n)
             leave(k, (4, 5), "scalar")
             store(k, (2,))
+            square_root(n)
             weights(c)
             flip(c, (0, 1, 2))
             group(c, (0,))
             flip(c, (3,))
             group(c, (1, 2, 3))
+            inverse(n)
+            spread(n)
             multiply(k, (6, 7))
             largest(c)
-            degrees(n)
-            square_root(n)
             leave(k, (6, 7), "scalar")
             store(k, (3,))
             quantise_w(c)
-            inverse(n)
             row_gain(c)
             multiply(c, (0, 1, 2, 3))
-            spread(n)
             regroup(n, "vector", G_COLS, D)
             mask(n)
 

@@ -26,8 +26,8 @@ BYTES = B * T * T * 2 + B * T * D * 2 + B * T * D * 4
 A_PITCH = T + P
 W_OFF = (0, 128, 384, 768)
 N_G = 2
-G_COLS = 768
-G_STEP = 256
+G_COLS = 832
+G_STEP = 416
 
 
 def tile_symbolicpenaltytracker_t_kernel(tc, A_rel, k_seq, out):
@@ -42,7 +42,6 @@ def tile_symbolicpenaltytracker_t_kernel(tc, A_rel, k_seq, out):
         wpool = ctx.enter_context(tc.tile_pool(name="wpool", bufs=2))
         cpool = ctx.enter_context(tc.tile_pool(name="cpool", bufs=3))
         kgpool = ctx.enter_context(tc.tile_pool(name="kgpool", bufs=1))
-        kvpool = ctx.enter_context(tc.tile_pool(name="kvpool", bufs=2))
         opool = ctx.enter_context(tc.tile_pool(name="opool", bufs=14))
         ps_b = ctx.enter_context(tc.psum_pool(name="ps_b", bufs=1))
         ps_t = ctx.enter_context(tc.psum_pool(name="ps_t", bufs=3))
@@ -61,11 +60,7 @@ def tile_symbolicpenaltytracker_t_kernel(tc, A_rel, k_seq, out):
                 )
             a_tiles.append(a_t)
             k_t = kpool.tile([P, 4, D], BF16, name="k_t")
-            for q in range(pieces):
-                cols = slice(q * D // pieces, (q + 1) * D // pieces)
-                nc.sync.dma_start(
-                    out=k_t[:, :, cols], in_=k_seq[b, :, cols].rearrange("(j p) d -> p j d", p=P)
-                )
+            nc.sync.dma_start(out=k_t[:], in_=k_seq[b].rearrange("(j p) d -> p j d", p=P))
             k_tiles.append(k_t)
 
         g_tiles = []
@@ -166,9 +161,10 @@ def tile_symbolicpenaltytracker_t_kernel(tc, A_rel, k_seq, out):
                     in_=w_t[(b, i)][:, 0 : i + 1, :].rearrange("p j t -> p t j"),
                 )
 
-        def largest(b):
-            mark[b] = small.tile([P, NT], F32, name="mark")
-            for i in range(NT):
+        def largest(b, tiles):
+            if b not in mark:
+                mark[b] = small.tile([P, NT], F32, name="mark")
+            for i in tiles:
                 nc.vector.tensor_reduce(
                     out=mark[b][:, i : i + 1],
                     in_=w_n[b][:, W_OFF[i] : W_OFF[i] + (i + 1) * P],
@@ -198,22 +194,10 @@ def tile_symbolicpenaltytracker_t_kernel(tc, A_rel, k_seq, out):
             )
             w_ops[b] = (w_codes, w_scales)
 
-        def piece(b, c0):
-            if b == 0:
-                if b not in k_g:
-                    k_g[b] = kgpool.tile([P, D, 4], BF16, name="k_first", align_bytes=64)
-                return k_g[b], 0
-            if c0 < G_COLS:
-                if (b, 0) not in k_g:
-                    k_g[(b, 0)] = kgpool.tile([P, G_COLS, 4], BF16, name="k_pool", align_bytes=64)
-                return k_g[(b, 0)], 0
-            if (b, 1) not in k_g:
-                k_g[(b, 1)] = kvpool.tile([P, D - G_COLS, 4], BF16, name="k_vec", align_bytes=64)
-            return k_g[(b, 1)], G_COLS
-
         def regroup(b, engine, c0, c1):
-            tile, first = piece(b, c0)
-            dst = tile[:, c0 - first : c1 - first, :]
+            if b not in k_g:
+                k_g[b] = kgpool.tile([P, D, 4], BF16, name="k_g", align_bytes=64)
+            dst = k_g[b][:, c0:c1, :]
             source = k_tiles[b][:, :, c0:c1]
             if engine == "gpsimd":
                 nc.gpsimd.tensor_scalar(
@@ -242,11 +226,10 @@ def tile_symbolicpenaltytracker_t_kernel(tc, A_rel, k_seq, out):
                 k_scales = cpool.tile([P, D], U8, name="k_scales", align_bytes=64)
                 k_ops[b] = (k_codes, k_scales)
             for c0, c1 in ranges:
-                tile, first = piece(b, c0)
                 nc.vector.quantize_mx(
                     out=k_ops[b][0][:, c0:c1].bitcast(FP8X4),
                     scales=k_ops[b][1][:, c0:c1],
-                    in_=tile[:, c0 - first : c1 - first, :].rearrange("p d t -> p (d t)"),
+                    in_=k_g[b][:, c0:c1, :].rearrange("p d t -> p (d t)"),
                 )
 
         def multiply(b, passes, pool=ps_o, name="acc"):
@@ -295,35 +278,34 @@ def tile_symbolicpenaltytracker_t_kernel(tc, A_rel, k_seq, out):
         mask(0)
         inverse(0)
         spread(0)
-        regroup_on_gpsimd(1)
-        regroup(0, "scalar", 0, HALF)
-        regroup(0, "vector", HALF, G_COLS)
         weights(0)
         flip(0, (0, 1, 2))
         group(0, (0,))
         flip(0, (3,))
         group(0, (1, 2, 3))
-        largest(0)
+        largest(0, range(NT))
+        regroup(0, "scalar", 0, HALF)
         degrees(1)
         square_root(1)
-        regroup(0, "vector", G_COLS, D)
-        quantise_k(0, ((0, HALF), (HALF, D)))
+        regroup(0, "vector", HALF, D)
         inverse(1)
         spread(1)
+        quantise_k(0, ((0, HALF), (HALF, D)))
         quantise_w(0)
         row_gain(0)
         multiply(0, (0, 1, 2, 3))
-        regroup(1, "vector", G_COLS, D)
+        regroup(1, "scalar", 0, HALF)
+        regroup(1, "vector", HALF, D)
         mask(1)
 
         for k in range(B - 2):
             c = k + 1
             n = k + 2
-            quantise_k(c, ((G_COLS, D), (0, HALF), (HALF, G_COLS)))
+            quantise_k(c, ((0, D),))
             regroup_on_gpsimd(n)
             leave(k, (0, 1, 2, 3), "scalar")
             store(k, (0, 1))
-            multiply(k, (4, 5))
+            multiply(k, (4, 5, 6, 7))
             degrees(n)
             leave(k, (4, 5), "scalar")
             store(k, (2,))
@@ -335,15 +317,14 @@ def tile_symbolicpenaltytracker_t_kernel(tc, A_rel, k_seq, out):
             group(c, (1, 2, 3))
             inverse(n)
             spread(n)
-            multiply(k, (6, 7))
-            largest(c)
+            largest(c, range(NT))
+            regroup(n, "scalar", G_COLS, D)
             leave(k, (6, 7), "scalar")
             store(k, (3,))
             quantise_w(c)
-            row_gain(c)
             multiply(c, (0, 1, 2, 3))
-            regroup(n, "vector", G_COLS, D)
             mask(n)
+            row_gain(c)
 
         k, c = B - 2, B - 1
         weights(c)
@@ -356,7 +337,7 @@ def tile_symbolicpenaltytracker_t_kernel(tc, A_rel, k_seq, out):
         flip(c, (3,))
         group(c, (1, 2, 3))
         multiply(k, (6, 7))
-        largest(c)
+        largest(c, range(NT))
         quantise_k(c, ((0, HALF),))
         leave(k, (5,), "vector")
         store(k, (2,))
@@ -364,7 +345,7 @@ def tile_symbolicpenaltytracker_t_kernel(tc, A_rel, k_seq, out):
         row_gain(c)
         leave(k, (6, 7), "scalar")
         store(k, (3,))
-        quantise_k(c, ((HALF, G_COLS), (G_COLS, D)))
+        quantise_k(c, ((HALF, D),))
         multiply(c, (0, 2, 4, 6))
         multiply(c, (1, 3, 5), ps_t, "w_t")
         multiply(c, (7,), ps_b, "row")

@@ -26,8 +26,8 @@ BYTES = B * T * T * 2 + B * T * D * 2 + B * T * D * 4
 A_PITCH = T + P
 W_OFF = (0, 128, 384, 768)
 N_G = 2
-G_COLS = 832
-G_STEP = 416
+G_COLS = 640
+G_STEP = 320
 
 
 def tile_symbolicpenaltytracker_t_kernel(tc, A_rel, k_seq, out):
@@ -305,51 +305,55 @@ def tile_symbolicpenaltytracker_t_kernel(tc, A_rel, k_seq, out):
             regroup_on_gpsimd(n)
             leave(k, (0, 1, 2, 3), "scalar")
             store(k, (0, 1))
-            multiply(k, (4, 5, 6, 7))
-            degrees(n)
-            leave(k, (4, 5), "scalar")
-            store(k, (2,))
-            square_root(n)
+            multiply(k, (4, 5))
             weights(c)
             flip(c, (0, 1, 2))
             group(c, (0,))
             flip(c, (3,))
             group(c, (1, 2, 3))
-            inverse(n)
-            spread(n)
+            multiply(k, (6, 7))
+            degrees(n)
+            square_root(n)
             largest(c, range(NT))
-            regroup(n, "scalar", G_COLS, D)
+            leave(k, (4, 5), "scalar")
+            store(k, (2,))
+            regroup(n, "scalar", 896, D)
             leave(k, (6, 7), "scalar")
             store(k, (3,))
+            inverse(n)
+            spread(n)
+            regroup(n, "vector", G_COLS, 896)
+            mask(n)
             quantise_w(c)
             multiply(c, (0, 1, 2, 3))
-            mask(n)
             row_gain(c)
 
         k, c = B - 2, B - 1
         weights(c)
-        leave(k, (0, 1, 2, 3), "scalar")
-        store(k, (0, 1))
-        multiply(k, (4, 5))
+        leave(k, (0, 1, 2), "scalar")
+        store(k, (0,))
         flip(c, (0, 1, 2))
-        leave(k, (4,), "scalar")
-        group(c, (0,))
+        group(c, (0, 1, 2))
+        multiply(k, (4, 5))
+        leave(k, (3,), "scalar")
+        store(k, (1,))
         flip(c, (3,))
-        group(c, (1, 2, 3))
+        group(c, (3,))
         multiply(k, (6, 7))
         largest(c, range(NT))
-        quantise_k(c, ((0, HALF),))
+        quantise_k(c, ((0, D),))
+        leave(k, (4,), "scalar")
         leave(k, (5,), "vector")
         store(k, (2,))
         quantise_w(c)
         row_gain(c)
-        leave(k, (6, 7), "scalar")
+        leave(k, (6,), "scalar")
+        leave(k, (7,), "vector")
         store(k, (3,))
-        quantise_k(c, ((HALF, D),))
-        multiply(c, (0, 2, 4, 6))
-        multiply(c, (1, 3, 5), ps_t, "w_t")
+        multiply(c, (0, 1, 2, 3))
+        multiply(c, (4, 5, 6), ps_t, "w_t")
         multiply(c, (7,), ps_b, "row")
         for i in range(NT):
-            leave(c, (2 * i + 1,), "vector")
             leave(c, (2 * i,), "scalar")
+            leave(c, (2 * i + 1,), "vector")
             store(c, (i,))

@@ -27,6 +27,7 @@ A_PITCH = T + P
 W_OFF = (0, 128, 384, 768)
 N_G = 2
 G_COLS = 640
+S_FIRST = 384
 G_STEP = 320
 
 
@@ -49,7 +50,8 @@ def tile_symbolicpenaltytracker_t_kernel(tc, A_rel, k_seq, out):
 
         a_tiles = []
         k_tiles = []
-        for b in range(B):
+
+        def load_a(b):
             a_t = apool.tile([P, NT * A_PITCH], BF16, name="a_t")
             pieces = 2 if b == 0 else 1
             for q in range(pieces):
@@ -59,9 +61,17 @@ def tile_symbolicpenaltytracker_t_kernel(tc, A_rel, k_seq, out):
                     in_=A_rel[b, q * n * P : (q + 1) * n * P, :].rearrange("(i p) s -> p i s", p=P),
                 )
             a_tiles.append(a_t)
+
+        def load_k(b):
             k_t = kpool.tile([P, 4, D], BF16, name="k_t")
             nc.sync.dma_start(out=k_t[:], in_=k_seq[b].rearrange("(j p) d -> p j d", p=P))
             k_tiles.append(k_t)
+
+        load_a(0)
+        for b in range(B):
+            if b + 1 < B:
+                load_a(b + 1)
+            load_k(b)
 
         g_tiles = []
         for n in range(N_G):
@@ -196,7 +206,7 @@ def tile_symbolicpenaltytracker_t_kernel(tc, A_rel, k_seq, out):
 
         def regroup(b, engine, c0, c1):
             if b not in k_g:
-                k_g[b] = kgpool.tile([P, D, 4], BF16, name="k_g", align_bytes=64)
+                k_g[b] = kgpool.tile([P, D, 4], BF16, name=("k_g" if b else "k_first"), align_bytes=64)
             dst = k_g[b][:, c0:c1, :]
             source = k_tiles[b][:, :, c0:c1]
             if engine == "gpsimd":
@@ -209,12 +219,13 @@ def tile_symbolicpenaltytracker_t_kernel(tc, A_rel, k_seq, out):
                     op1=ALU.add,
                 )
                 return
-            dst = dst.rearrange("p (c i) t -> p c t i", i=4)
-            source = source.rearrange("p t (c i) -> p c t i", i=4)
             if engine == "scalar":
-                nc.scalar.copy(out=dst, in_=source)
-            else:
-                nc.vector.tensor_copy(out=dst, in_=source)
+                nc.scalar.copy(out=dst, in_=source.rearrange("p t c -> p c t"))
+                return
+            nc.vector.tensor_copy(
+                out=dst.rearrange("p (c i) t -> p c t i", i=4),
+                in_=source.rearrange("p t (c i) -> p c t i", i=4),
+            )
 
         def regroup_on_gpsimd(b):
             for c0 in range(0, G_COLS, G_STEP):
@@ -278,25 +289,25 @@ def tile_symbolicpenaltytracker_t_kernel(tc, A_rel, k_seq, out):
         mask(0)
         inverse(0)
         spread(0)
+        degrees(1)
+        square_root(1)
         weights(0)
         flip(0, (0, 1, 2))
         group(0, (0,))
         flip(0, (3,))
         group(0, (1, 2, 3))
-        largest(0, range(NT))
-        regroup(0, "scalar", 0, HALF)
-        degrees(1)
-        square_root(1)
-        regroup(0, "vector", HALF, D)
         inverse(1)
         spread(1)
-        quantise_k(0, ((0, HALF), (HALF, D)))
+        mask(1)
+        largest(0, range(NT))
+        regroup(0, "scalar", 0, S_FIRST)
+        regroup(0, "vector", S_FIRST, D)
+        quantise_k(0, ((0, D),))
         quantise_w(0)
         row_gain(0)
         multiply(0, (0, 1, 2, 3))
-        regroup(1, "scalar", 0, HALF)
-        regroup(1, "vector", HALF, D)
-        mask(1)
+        regroup(1, "scalar", 0, 512)
+        regroup(1, "vector", 512, D)
 
         for k in range(B - 2):
             c = k + 1
@@ -317,12 +328,12 @@ def tile_symbolicpenaltytracker_t_kernel(tc, A_rel, k_seq, out):
             largest(c, range(NT))
             leave(k, (4, 5), "scalar")
             store(k, (2,))
-            regroup(n, "scalar", 896, D)
+            regroup(n, "scalar", 832, D)
             leave(k, (6, 7), "scalar")
             store(k, (3,))
             inverse(n)
             spread(n)
-            regroup(n, "vector", G_COLS, 896)
+            regroup(n, "vector", G_COLS, 832)
             mask(n)
             quantise_w(c)
             multiply(c, (0, 1, 2, 3))

@@ -26,9 +26,9 @@ BYTES = B * T * T * 2 + B * T * D * 2 + B * T * D * 4
 A_PITCH = T + P
 W_OFF = (0, 128, 384, 768)
 N_G = 2
-G_COLS = 640
+G_COLS = 704
 S_FIRST = 384
-G_STEP = 320
+G_STEP = 352
 
 
 def tile_symbolicpenaltytracker_t_kernel(tc, A_rel, k_seq, out):
@@ -73,13 +73,16 @@ def tile_symbolicpenaltytracker_t_kernel(tc, A_rel, k_seq, out):
                 load_a(b + 1)
             load_k(b)
 
+        eps_t = const.tile([P, 1], F32, name="eps_t")
+        nc.vector.memset(eps_t[:], EPS)
+        warm_t = const.tile([P, 1], F32, name="warm_t")
+        nc.scalar.activation(out=warm_t[:], in_=eps_t[:], func=ACT.Sqrt)
+
         g_tiles = []
         for n in range(N_G):
             g_t = const.tile([P, NT, P, 4], BF16, name="g_t%d" % n, align_bytes=64)
             nc.vector.memset(g_t[:].rearrange("p i t j -> p (i t j)").bitcast(U32), 0)
             g_tiles.append(g_t)
-        eps_t = const.tile([P, 1], F32, name="eps_t")
-        nc.vector.memset(eps_t[:], EPS)
         ident = const.tile([P, P], F32, name="ident")
         make_identity(nc, ident[:])
         tri_f = const.tile([P, P], F32, name="tri_f")
@@ -99,9 +102,10 @@ def tile_symbolicpenaltytracker_t_kernel(tc, A_rel, k_seq, out):
         deg, root, dis, dis_b, w_n, w_t = {}, {}, {}, {}, {}, {}
         mark, gain, w_ops, k_g, k_ops, acc, o_t = {}, {}, {}, {}, {}, {}, {}
 
-        def degrees(b):
-            deg[b] = small.tile([P, NT], F32, name="deg")
-            for i in range(NT):
+        def degrees(b, tiles):
+            if b not in deg:
+                deg[b] = small.tile([P, NT], F32, name="deg")
+            for i in tiles:
                 junk = junkp.tile([P, T], BF16, name="d_junk")
                 nc.vector.tensor_scalar(
                     out=junk[:],
@@ -110,6 +114,16 @@ def tile_symbolicpenaltytracker_t_kernel(tc, A_rel, k_seq, out):
                     scalar2=None,
                     op0=ALU.mult,
                     op1=ALU.add,
+                    accum_out=deg[b][:, i : i + 1],
+                )
+
+        def degrees_on_scalar(b, tiles):
+            for i in tiles:
+                junk = junkp.tile([P, T], BF16, name="s_junk")
+                nc.scalar.activation(
+                    out=junk[:],
+                    in_=a_tiles[b][:, i * T : (i + 1) * T],
+                    func=ACT.Copy,
                     accum_out=deg[b][:, i : i + 1],
                 )
 
@@ -284,24 +298,27 @@ def tile_symbolicpenaltytracker_t_kernel(tc, A_rel, k_seq, out):
             for i in tiles:
                 nc.sync.dma_start(out=out[b, i * P : (i + 1) * P, :], in_=o_t[(b, i)][:])
 
-        degrees(0)
+        degrees(0, (0, 1, 2))
+        degrees_on_scalar(0, (3,))
         square_root(0)
         mask(0)
         inverse(0)
         spread(0)
-        degrees(1)
+        degrees(1, (0, 1))
+        degrees_on_scalar(1, (2, 3))
         square_root(1)
+        regroup(0, "gpsimd", 0, 320)
         weights(0)
         flip(0, (0, 1, 2))
         group(0, (0,))
         flip(0, (3,))
         group(0, (1, 2, 3))
+        largest(0, range(NT))
         inverse(1)
         spread(1)
         mask(1)
-        largest(0, range(NT))
-        regroup(0, "scalar", 0, S_FIRST)
-        regroup(0, "vector", S_FIRST, D)
+        regroup(0, "scalar", 320, 448)
+        regroup(0, "vector", 448, D)
         quantise_k(0, ((0, D),))
         quantise_w(0)
         row_gain(0)
@@ -323,17 +340,17 @@ def tile_symbolicpenaltytracker_t_kernel(tc, A_rel, k_seq, out):
             flip(c, (3,))
             group(c, (1, 2, 3))
             multiply(k, (6, 7))
-            degrees(n)
+            degrees(n, range(NT))
             square_root(n)
             largest(c, range(NT))
             leave(k, (4, 5), "scalar")
             store(k, (2,))
-            regroup(n, "scalar", 832, D)
+            regroup(n, "scalar", 928, D)
             leave(k, (6, 7), "scalar")
             store(k, (3,))
             inverse(n)
             spread(n)
-            regroup(n, "vector", G_COLS, 832)
+            regroup(n, "vector", G_COLS, 928)
             mask(n)
             quantise_w(c)
             multiply(c, (0, 1, 2, 3))
@@ -341,20 +358,20 @@ def tile_symbolicpenaltytracker_t_kernel(tc, A_rel, k_seq, out):
 
         k, c = B - 2, B - 1
         weights(c)
-        leave(k, (0, 1, 2), "scalar")
-        store(k, (0,))
         flip(c, (0, 1, 2))
-        group(c, (0, 1, 2))
+        leave(k, (0, 1), "scalar")
+        store(k, (0,))
         multiply(k, (4, 5))
-        leave(k, (3,), "scalar")
-        store(k, (1,))
+        group(c, (0, 1, 2))
+        leave(k, (2,), "scalar")
         flip(c, (3,))
         group(c, (3,))
-        multiply(k, (6, 7))
         largest(c, range(NT))
+        leave(k, (3,), "vector")
+        store(k, (1,))
+        multiply(k, (6, 7))
         quantise_k(c, ((0, D),))
-        leave(k, (4,), "scalar")
-        leave(k, (5,), "vector")
+        leave(k, (4, 5), "scalar")
         store(k, (2,))
         quantise_w(c)
         row_gain(c)

@@ -218,7 +218,7 @@ def tile_symbolicpenaltytracker_t_kernel(tc, A_rel, k_seq, out):
             )
             w_ops[b] = (w_codes, w_scales)
 
-        def regroup(b, engine, c0, c1):
+        def regroup(b, engine, c0, c1, one=1.0):
             if b not in k_g:
                 k_g[b] = kgpool.tile([P, D, 4], BF16, name=("k_g" if b else "k_first"), align_bytes=64)
             dst = k_g[b][:, c0:c1, :]
@@ -227,7 +227,7 @@ def tile_symbolicpenaltytracker_t_kernel(tc, A_rel, k_seq, out):
                 nc.gpsimd.tensor_scalar(
                     out=dst,
                     in0=source.rearrange("p t c -> p c t"),
-                    scalar1=1.0,
+                    scalar1=one,
                     scalar2=0.0,
                     op0=ALU.mult,
                     op1=ALU.add,
@@ -316,9 +316,9 @@ def tile_symbolicpenaltytracker_t_kernel(tc, A_rel, k_seq, out):
         largest(0, range(NT))
         inverse(1)
         spread(1)
-        mask(1)
         regroup(0, "scalar", 320, 448)
         regroup(0, "vector", 448, D)
+        mask(1)
         quantise_k(0, ((0, D),))
         quantise_w(0)
         row_gain(0)
@@ -333,9 +333,9 @@ def tile_symbolicpenaltytracker_t_kernel(tc, A_rel, k_seq, out):
             regroup_on_gpsimd(n)
             leave(k, (0, 1, 2, 3), "scalar")
             store(k, (0, 1))
-            multiply(k, (4, 5))
             weights(c)
             flip(c, (0, 1, 2))
+            multiply(k, (4, 5))
             group(c, (0,))
             flip(c, (3,))
             group(c, (1, 2, 3))
@@ -345,18 +345,25 @@ def tile_symbolicpenaltytracker_t_kernel(tc, A_rel, k_seq, out):
             largest(c, range(NT))
             leave(k, (4, 5), "scalar")
             store(k, (2,))
-            regroup(n, "scalar", 928, D)
+            if n < B - 1:
+                regroup(n, "scalar", 928, D)
             leave(k, (6, 7), "scalar")
             store(k, (3,))
             inverse(n)
             spread(n)
-            regroup(n, "vector", G_COLS, 928)
+            if n < B - 1:
+                regroup(n, "vector", G_COLS, 928)
             mask(n)
             quantise_w(c)
             multiply(c, (0, 1, 2, 3))
             row_gain(c)
 
         k, c = B - 2, B - 1
+        go = small.tile([P, 1], F32, name="go")
+        nc.vector.tensor_scalar(
+            out=go[:], in0=eps_t[:], scalar1=0.0, scalar2=1.0, op0=ALU.mult, op1=ALU.add
+        )
+        regroup(c, "gpsimd", G_COLS, D, go[:])
         weights(c)
         flip(c, (0, 1, 2))
         leave(k, (0, 1), "scalar")

from contextlib import ExitStack
import math

import concourse.mybir as mybir
from concourse.masks import make_identity

F32 = mybir.dt.float32
BF16 = mybir.dt.bfloat16
U32 = mybir.dt.uint32
U8 = mybir.dt.uint8
FP8X4 = mybir.dt.float8_e4m3fn_x4
ALU = mybir.AluOpType
ACT = mybir.ActivationFunctionType
AX = mybir.AxisListType

B, T, D = 8, 512, 1024
P = 128
NT = T // P
HALF = 512
EPS = 1e-06
REL_THRESH = 1e-09
GAMMA = 0.5
FLOPS = 2 * B * T * T * D
BYTES = B * T * T * 2 + B * T * D * 2 + B * T * D * 4

A_PITCH = T + P
W_OFF = (0, 128, 384, 768)
N_G = 2
G_COLS = 704
S_FIRST = 384
G_STEP = 352


def tile_symbolicpenaltytracker_t_kernel(tc, A_rel, k_seq, out):
    nc = tc.nc
    with ExitStack() as ctx:
        ctx.enter_context(tc.manual_schedule())
        const = ctx.enter_context(tc.tile_pool(name="const", bufs=1))
        apool = ctx.enter_context(tc.tile_pool(name="apool", bufs=B))
        kpool = ctx.enter_context(tc.tile_pool(name="kpool", bufs=B))
        junkp = ctx.enter_context(tc.tile_pool(name="junkp", bufs=2))
        small = ctx.enter_context(tc.tile_pool(name="small", bufs=3))
        wpool = ctx.enter_context(tc.tile_pool(name="wpool", bufs=2))
        cpool = ctx.enter_context(tc.tile_pool(name="cpool", bufs=3))
        kgpool = ctx.enter_context(tc.tile_pool(name="kgpool", bufs=1))
        opool = ctx.enter_context(tc.tile_pool(name="opool", bufs=14))
        ps_b = ctx.enter_context(tc.psum_pool(name="ps_b", bufs=1))
        ps_t = ctx.enter_context(tc.psum_pool(name="ps_t", bufs=3))
        ps_o = ctx.enter_context(tc.psum_pool(name="ps_o", bufs=4))

        a_tiles = []
        k_tiles = []

        def load_a(b):
            a_t = apool.tile([P, NT * A_PITCH], BF16, name="a_t")
            pieces = 2 if b == 0 else 1
            for q in range(pieces):
                n = NT // pieces
                nc.sync.dma_start(
                    out=a_t[:, q * n * T : (q + 1) * n * T].rearrange("p (i s) -> p i s", i=n),
                    in_=A_rel[b, q * n * P : (q + 1) * n * P, :].rearrange("(i p) s -> p i s", p=P),
                )
            a_tiles.append(a_t)

        def load_k(b):
            k_t = kpool.tile([P, 4, D], BF16, name="k_t")
            nc.sync.dma_start(out=k_t[:], in_=k_seq[b].rearrange("(j p) d -> p j d", p=P))
            k_tiles.append(k_t)

        load_a(0)
        for b in range(B):
            if b + 1 < B:
                load_a(b + 1)
            load_k(b)

        eps_t = const.tile([P, 1], F32, name="eps_t")
        nc.vector.memset(eps_t[:], EPS)
        warm_t = const.tile([P, 1], F32, name="warm_t")
        nc.scalar.activation(out=warm_t[:], in_=eps_t[:], func=ACT.Sqrt)

        g_tiles = []
        for n in range(N_G):
            g_t = const.tile([P, NT, P, 4], BF16, name="g_t%d" % n, align_bytes=64)
            nc.vector.memset(g_t[:].rearrange("p i t j -> p (i t j)").bitcast(U32), 0)
            g_tiles.append(g_t)
        ident = const.tile([P, P], F32, name="ident")
        make_identity(nc, ident[:])
        tri_f = const.tile([P, P], F32, name="tri_f")
        nc.gpsimd.memset(tri_f[:], 1.0)
        nc.gpsimd.affine_select(
            out=tri_f[:],
            in_=tri_f[:],
            compare_op=ALU.is_ge,
            fill=0.0,
            base=0,
            pattern=[[-1, P]],
            channel_multiplier=1,
        )
        tri_b = const.tile([P, P], BF16, name="tri_b")
        nc.vector.tensor_copy(out=tri_b[:], in_=tri_f[:])

        deg, root, dis, dis_b, w_n, w_t = {}, {}, {}, {}, {}, {}
        mark, gain, w_ops, k_g, k_ops, acc, o_t = {}, {}, {}, {}, {}, {}, {}

        def degrees(b, tiles):
            if b not in deg:
                deg[b] = small.tile([P, NT], F32, name="deg")
            for i in tiles:
                junk = junkp.tile([P, T], BF16, name="d_junk")
                nc.vector.tensor_scalar(
                    out=junk[:],
                    in0=a_tiles[b][:, i * T : (i + 1) * T],
                    scalar1=1.0,
                    scalar2=None,
                    op0=ALU.mult,
                    op1=ALU.add,
                    accum_out=deg[b][:, i : i + 1],
                )

        def degrees_on_scalar(b, tiles):
            for i in tiles:
                junk = junkp.tile([P, T], BF16, name="s_junk")
                nc.scalar.activation(
                    out=junk[:],
                    in_=a_tiles[b][:, i * T : (i + 1) * T],
                    func=ACT.Copy,
                    accum_out=deg[b][:, i : i + 1],
                )

        def square_root(b):
            root[b] = small.tile([P, NT], F32, name="root")
            nc.scalar.activation(
                out=root[b][:], in_=deg[b][:], func=ACT.Sqrt, bias=eps_t[:], scale=1.0
            )

        def inverse(b):
            dis[b] = small.tile([P, NT], F32, name="dis")
            nc.vector.reciprocal(out=dis[b][:], in_=root[b][:])

        def mask(b):
            diag = a_tiles[b][:].rearrange("p (i c) -> p i c", c=A_PITCH)[:, :, 0:P]
            nc.vector.tensor_tensor(
                out=diag,
                in0=diag,
                in1=tri_b[:].unsqueeze(1).to_broadcast([P, NT, P]),
                op=ALU.mult,
            )

        def spread(b):
            dis_b[b] = ps_b.tile([P, T], F32, name="row")
            for i in range(NT):
                nc.tensor.transpose(
                    out=dis_b[b][:, i * P : (i + 1) * P],
                    in_=dis[b][:, i : i + 1].to_broadcast([P, P]),
                    identity=ident[:],
                )

        def weights(b):
            w_n[b] = wpool.tile([P, 1280], F32, name="w_n")
            for i in range(NT):
                width = (i + 1) * P
                nc.vector.scalar_tensor_tensor(
                    out=w_n[b][:, W_OFF[i] : W_OFF[i] + width],
                    in0=a_tiles[b][:, i * T : i * T + width],
                    scalar=dis[b][:, i : i + 1],
                    in1=dis_b[b][:, 0:width],
                    op0=ALU.mult,
                    op1=ALU.mult,
                )

        def flip(b, tiles):
            for i in tiles:
                w_t[(b, i)] = ps_t.tile([P, 4, P], F32, name="w_t")
                for j in range(i + 1):
                    nc.tensor.transpose(
                        out=w_t[(b, i)][:, j, :],
                        in_=w_n[b][:, W_OFF[i] + j * P : W_OFF[i] + (j + 1) * P],
                        identity=ident[:],
                    )

        def group(b, tiles):
            for i in tiles:
                nc.scalar.copy(
                    out=g_tiles[b % N_G][:, i, :, 0 : i + 1],
                    in_=w_t[(b, i)][:, 0 : i + 1, :].rearrange("p j t -> p t j"),
                )

        def largest(b, tiles):
            if b not in mark:
                mark[b] = small.tile([P, NT], F32, name="mark")
            for i in tiles:
                nc.vector.tensor_reduce(
                    out=mark[b][:, i : i + 1],
                    in_=w_n[b][:, W_OFF[i] : W_OFF[i] + (i + 1) * P],
                    axis=AX.X,
                    op=ALU.max,
                    apply_absolute_value=True,
                )

        def row_gain(b):
            gain[b] = small.tile([P, NT], F32, name="gain")
            nc.vector.tensor_scalar(
                out=gain[b][:],
                in0=mark[b][:],
                scalar1=REL_THRESH,
                scalar2=math.sqrt(GAMMA),
                op0=ALU.is_gt,
                op1=ALU.mult,
            )

        def quantise_w(b):
            w_codes = cpool.tile([P, T], U32, name="w_codes", align_bytes=64)
            w_scales = cpool.tile([P, T], U8, name="w_scales", align_bytes=64)
            nc.vector.quantize_mx(
                out=w_codes[:].bitcast(FP8X4),
                scales=w_scales[:],
                in_=g_tiles[b % N_G][:].rearrange("p i t j -> p (i t j)"),
            )
            w_ops[b] = (w_codes, w_scales)

        def regroup(b, engine, c0, c1, one=1.0):
            if b not in k_g:
                k_g[b] = kgpool.tile([P, D, 4], BF16, name=("k_g" if b else "k_first"), align_bytes=64)
            dst = k_g[b][:, c0:c1, :]
            source = k_tiles[b][:, :, c0:c1]
            if engine == "gpsimd":
                nc.gpsimd.tensor_scalar(
                    out=dst,
                    in0=source.rearrange("p t c -> p c t"),
                    scalar1=one,
                    scalar2=0.0,
                    op0=ALU.mult,
                    op1=ALU.add,
                )
                return
            if engine == "scalar":
                nc.scalar.copy(out=dst, in_=source.rearrange("p t c -> p c t"))
                return
            nc.vector.tensor_copy(
                out=dst.rearrange("p (c i) t -> p c t i", i=4),
                in_=source.rearrange("p t (c i) -> p c t i", i=4),
            )

        def regroup_on_gpsimd(b):
            for c0 in range(0, G_COLS, G_STEP):
                regroup(b, "gpsimd", c0, c0 + G_STEP)

        def quantise_k(b, ranges):
            if b not in k_ops:
                k_codes = cpool.tile([P, D], U32, name="k_codes", align_bytes=64)
                k_scales = cpool.tile([P, D], U8, name="k_scales", align_bytes=64)
                k_ops[b] = (k_codes, k_scales)
            for c0, c1 in ranges:
                nc.vector.quantize_mx(
                    out=k_ops[b][0][:, c0:c1].bitcast(FP8X4),
                    scales=k_ops[b][1][:, c0:c1],
                    in_=k_g[b][:, c0:c1, :].rearrange("p d t -> p (d t)"),
                )

        def multiply(b, passes, pool=ps_o, name="acc"):
            for n in passes:
                rows = slice((n // 2) * P, (n // 2 + 1) * P)
                cols = slice((n % 2) * HALF, (n % 2 + 1) * HALF)
                acc[(b, n)] = pool.tile([P, HALF], F32, name=name)
                nc.tensor.matmul_mx(
                    out=acc[(b, n)][:],
                    lhsT=w_ops[b][0][:, rows].bitcast(FP8X4),
                    lhsT_scale=w_ops[b][1][:, rows],
                    rhs=k_ops[b][0][:, cols].bitcast(FP8X4),
                    rhs_scale=k_ops[b][1][:, cols],
                    start=True,
                    stop=True,
                )

        def leave(b, passes, engine):
            for n in passes:
                i = n // 2
                cols = slice((n % 2) * HALF, (n % 2 + 1) * HALF)
                if (b, i) not in o_t:
                    o_t[(b, i)] = opool.tile([P, D], F32, name="o_t")
                if engine == "vector":
                    nc.vector.tensor_scalar(
                        out=o_t[(b, i)][:, cols],
                        in0=acc[(b, n)][:],
                        scalar1=gain[b][:, i : i + 1],
                        scalar2=None,
                        op0=ALU.mult,
                    )
                else:
                    nc.scalar.activation(
                        out=o_t[(b, i)][:, cols],
                        in_=acc[(b, n)][:],
                        func=ACT.Copy,
                        scale=gain[b][:, i : i + 1],
                    )

        def store(b, tiles):
            for i in tiles:
                nc.sync.dma_start(out=out[b, i * P : (i + 1) * P, :], in_=o_t[(b, i)][:])

        degrees(0, (0, 1, 2))
        degrees_on_scalar(0, (3,))
        square_root(0)
        mask(0)
        inverse(0)
        spread(0)
        degrees(1, (0, 1))
        degrees_on_scalar(1, (2, 3))
        square_root(1)
        regroup(0, "gpsimd", 0, 320)
        weights(0)
        flip(0, (0, 1, 2))
        group(0, (0,))
        flip(0, (3,))
        group(0, (1, 2, 3))
        largest(0, range(NT))
        inverse(1)
        spread(1)
        regroup(0, "scalar", 320, 448)
        regroup(0, "vector", 448, D)
        mask(1)
        quantise_k(0, ((0, D),))
        quantise_w(0)
        row_gain(0)
        multiply(0, (0, 1, 2, 3))
        regroup(1, "scalar", 0, 512)
        regroup(1, "vector", 512, D)

        for k in range(B - 2):
            c = k + 1
            n = k + 2
            quantise_k(c, ((0, D),))
            regroup_on_gpsimd(n)
            leave(k, (0, 1, 2, 3), "scalar")
            store(k, (0, 1))
            weights(c)
            flip(c, (0, 1, 2))
            multiply(k, (4, 5))
            group(c, (0,))
            flip(c, (3,))
            group(c, (1, 2, 3))
            multiply(k, (6, 7))
            degrees(n, range(NT))
            square_root(n)
            largest(c, range(NT))
            leave(k, (4, 5), "scalar")
            store(k, (2,))
            if n < B - 1:
                regroup(n, "scalar", 928, D)
            leave(k, (6, 7), "scalar")
            store(k, (3,))
            inverse(n)
            spread(n)
            if n < B - 1:
                regroup(n, "vector", G_COLS, 928)
            mask(n)
            quantise_w(c)
            multiply(c, (0, 1, 2, 3))
            row_gain(c)

        k, c = B - 2, B - 1
        go = small.tile([P, 1], F32, name="go")
        nc.vector.tensor_scalar(
            out=go[:], in0=eps_t[:], scalar1=0.0, scalar2=1.0, op0=ALU.mult, op1=ALU.add
        )
        regroup(c, "gpsimd", G_COLS, D, go[:])
        weights(c)
        flip(c, (0, 1, 2))
        leave(k, (0, 1), "scalar")
        store(k, (0,))
        multiply(k, (4, 5))
        group(c, (0, 1, 2))
        leave(k, (2,), "scalar")
        flip(c, (3,))
        group(c, (3,))
        largest(c, range(NT))
        leave(k, (3,), "vector")
        store(k, (1,))
        multiply(k, (6, 7))
        quantise_k(c, ((0, D),))
        leave(k, (4, 5), "scalar")
        store(k, (2,))
        quantise_w(c)
        row_gain(c)
        leave(k, (6,), "scalar")
        leave(k, (7,), "vector")
        store(k, (3,))
        multiply(c, (0, 1, 2, 3))
        multiply(c, (4, 5, 6), ps_t, "w_t")
        multiply(c, (7,), ps_b, "row")
        for i in range(NT):
            leave(c, (2 * i,), "scalar")
            leave(c, (2 * i + 1,), "vector")
            store(c, (i,))
